import numpy as np
import ml_dtypes


def mxq(x, axis, fmt="e4m3"):
    dtype, down = {"e4m3": (ml_dtypes.float8_e4m3fn, 7), "e5m2": (ml_dtypes.float8_e5m2, 14)}[fmt]
    v = np.moveaxis(np.asarray(x, np.float32).astype(ml_dtypes.bfloat16).astype(np.float64), axis, -1)
    blocks = v.reshape(v.shape[:-1] + (-1, 32))
    amax = np.abs(blocks).max(-1, keepdims=True)
    byte = np.maximum(np.where(amax > 0, np.frexp(amax)[1] - 1 + 127, 0) - down, 1)
    scale = np.exp2(byte - 127.0)
    codes = (blocks / scale).astype(np.float32).astype(dtype).astype(np.float64)
    return np.moveaxis((codes * scale).reshape(v.shape), -1, axis)


WIDE = False


def mx_kscale(k):
    if not WIDE:
        return np.ones(k)
    levels = np.array([10, -10, 5, -5, 0])
    a = np.random.permutation(np.resize(levels, k // 512 * 4)).reshape(k // 512, 4)
    idx = np.arange(k)
    return np.exp2(a[idx // 512, idx % 128 // 32])


BF16 = ml_dtypes.bfloat16


def bf(x):
    return np.asarray(x, np.float32).astype(BF16)


def f64(x):
    return np.asarray(x).astype(np.float64)


B, C, H, W, G0, G1, G2, HF, DO = 32, 256, 4, 4, 1024, 128, 512, 512, 256
N = H * W


def relative_grid_feat():
    oh = f64(np.repeat(np.arange(H), W))
    ow = f64(np.tile(np.arange(W), H))
    rel = np.stack([oh[:, None] - oh[None, :], ow[:, None] - ow[None, :]], axis=-1)
    return rel - rel.mean()


def setup_inputs():
    s = mx_kscale(2 * C)[:C]
    t = mx_kscale(G0)
    w_obj = np.random.standard_normal((2 * C, G0)) / np.sqrt(2 * C) / np.concatenate([s, s])[:, None]
    w_rel = np.random.standard_normal((2, G0)) * 1.5 / np.sqrt(H * H + W * W)
    return {"x": bf(np.random.standard_normal((B, C, H, W)) * s[None, :, None, None]),
            "g_W0": bf(np.concatenate([w_obj, w_rel], axis=0) * t),
            "g_b0": bf(np.random.standard_normal(G0) * 0.2 * t),
            "g_W1": bf(np.random.standard_normal((G0, G1)) / np.sqrt(G0) / t[:, None]),
            "g_b1": bf(np.random.standard_normal(G1) * 0.2)}


def reference(x, g_W0, g_b0, g_W1, g_b1):
    xT = f64(x).reshape(B, C, N).transpose(0, 2, 1)
    xi = np.broadcast_to(xT[:, None, :, :], (B, N, N, C))
    xj = np.broadcast_to(xT[:, :, None, :], (B, N, N, C))
    pair = np.concatenate([xi, xj], axis=-1)
    w0 = f64(g_W0)
    rel = relative_grid_feat()
    pos = rel[:, :, 0, None] * w0[2 * C] + rel[:, :, 1, None] * w0[2 * C + 1]
    h0 = np.maximum((mxq(pair, 3, "e4m3") @ mxq(w0[:2 * C], 0, "e4m3")) + pos + f64(g_b0), 0.0)
    return np.maximum((mxq(h0, 3, "e4m3") @ mxq(f64(g_W1), 0, "e4m3")) + f64(g_b1), 0.0)

@@ -1,0 +1,238 @@
+from contextlib import ExitStack
+
+import concourse.bass as bass
+import concourse.mybir as mybir
+import concourse.tile as tile
+from concourse.masks import make_identity
+
+F32 = mybir.dt.float32
+BF16 = mybir.dt.bfloat16
+U32 = mybir.dt.uint32
+U8 = mybir.dt.uint8
+I32 = mybir.dt.int32
+FP8X4 = mybir.dt.float8_e4m3fn_x4
+ACT = mybir.ActivationFunctionType
+ALU = mybir.AluOpType
+
+P = 128
+B = 32
+CELLS = 16
+G0 = 1024
+G1 = 128
+GT = G0 // P
+COLS = CELLS * B
+NPB = 3
+REL_MEAN = 0.0
+
+FLOPS = 2 * B * CELLS * CELLS * (512 * G0 + G0 * G1)
+
+
+def shift_groups(a, d):
+    found = [(a, d, 0, 4 - a, 0, 4 - d)]
+    if d > 0 and a < 3:
+        found.append((a + 1, d - 4, 0, 3 - a, 4 - d, 4))
+    if a > 0:
+        found.append((a - 4, d, 4 - a, 4, 0, 4 - d))
+    if d > 0:
+        found.append((a - 3, d - 4, 3 - a, 4, 4 - d, 4))
+    return found
+
+
+def tile_relationnetwork_pa_t_kernel(tc, x, g_W0, g_b0, g_W1, g_b1, out):
+    nc = tc.nc
+    with ExitStack() as ctx:
+        keep = ctx.enter_context(tc.tile_pool(name="keep", bufs=1))
+        planes = ctx.enter_context(tc.tile_pool(name="planes", bufs=4))
+        grouped = ctx.enter_context(tc.tile_pool(name="grouped", bufs=3))
+        packed = ctx.enter_context(tc.tile_pool(name="packed", bufs=4))
+        results = ctx.enter_context(tc.tile_pool(name="results", bufs=3))
+        psum1 = ctx.enter_context(tc.psum_pool(name="psum1", bufs=6))
+        psum2 = ctx.enter_context(tc.psum_pool(name="psum2", bufs=2))
+
+        xraw = keep.tile([P, B, 64], BF16)
+        xv = x.rearrange("b (p j) h w -> p b (j h w)", j=4)
+        nc.sync.dma_start(out=xraw[0:64], in_=xv)
+        nc.sync.dma_start(out=xraw[64:128], in_=xv)
+        w0raw = keep.tile([P, 4, G0], BF16)
+        for h in range(2):
+            nc.sync.dma_start(
+                out=w0raw[:, :, h * 512 : (h + 1) * 512],
+                in_=g_W0[0:512, h * 512 : (h + 1) * 512].rearrange("(p j) g -> p j g", j=4),
+            )
+        w1raw = keep.tile([P, GT, G1], BF16)
+        nc.sync.dma_start(out=w1raw[:], in_=g_W1.rearrange("(u p) n -> p u n", p=P))
+
+        brow = keep.tile([P, P], BF16)
+        nc.vector.memset(brow[:], 0.0)
+        nc.scalar.dma_start(out=brow[0:8, :], in_=g_b0.rearrange("(u g) -> u g", g=P))
+        nc.scalar.dma_start(out=brow[8:24, :], in_=g_W0[512:514, :].rearrange("v (u g) -> (v u) g", g=P))
+        b1bc = keep.tile([P, G1], BF16)
+        nc.scalar.dma_start(out=b1bc[:], in_=g_b1.partition_broadcast(P))
+
+        ident = keep.tile([P, P], BF16)
+        make_identity(nc, ident[:])
+        delta = keep.tile([P, 7, GT], F32)
+        for i in range(7):
+            nc.gpsimd.memset(delta[:, i, :], float(i - 3) - REL_MEAN)
+
+        ow = keep.tile([P, COLS], U32, align_bytes=64)
+        osc = keep.tile([P, COLS], U8, align_bytes=64)
+        nc.vector.memset(osc[:].bitcast(I32), 0)
+
+        xg = keep.tile([P, CELLS, B, 4], BF16, align_bytes=64)
+        xr = xraw[:].rearrange("p b (j n) -> p n b j", j=4)
+        nc.vector.tensor_copy(out=xg[:, 0:8], in_=xr[:, 0:8])
+        nc.scalar.copy(out=xg[:, 8:16], in_=xr[:, 8:16])
+
+        w0g = keep.tile([P, G0, 4], BF16, align_bytes=64)
+        w0w = keep.tile([P, G0], U32, align_bytes=64)
+        w0s = keep.tile([P, G0], U8, align_bytes=64)
+
+        def w0_regroup(engine_copy, h):
+            cols = slice(h * 256, (h + 1) * 256)
+            engine_copy(
+                out=w0g[:, cols, :].rearrange("p (c i) j -> p c j i", i=4),
+                in_=w0raw[:, :, cols].rearrange("p j (c i) -> p c j i", i=4),
+            )
+
+        def w0_quantise(h):
+            cols = slice(h * 256, (h + 1) * 256)
+            nc.vector.quantize_mx(
+                out=w0w[:, cols].bitcast(FP8X4),
+                scales=w0s[:, cols],
+                in_=w0g[:, cols, :].rearrange("p g j -> p (g j)"),
+            )
+
+        w0_regroup(nc.vector.tensor_copy, 0)
+        w0_regroup(nc.scalar.copy, 1)
+        nc.vector.quantize_mx(
+            out=ow[:].bitcast(FP8X4), scales=osc[:], in_=xg[:].rearrange("p n b j -> p (n b j)")
+        )
+        w0_quantise(0)
+        w0_regroup(nc.vector.tensor_copy, 2)
+        w0_regroup(nc.scalar.copy, 3)
+        w0_quantise(1)
+        w0_quantise(2)
+        w0_quantise(3)
+
+        bt_ps = psum2.tile([P, P], BF16, tag="l2")
+        nc.tensor.transpose(bt_ps[:], brow[:], ident[:])
+        bt = keep.tile([P, 24], F32)
+        nc.vector.tensor_copy(out=bt[:], in_=bt_ps[:, 0:24])
+        row_part = keep.tile([P, 7, GT], F32)
+        col_part = keep.tile([P, 7, GT], F32)
+        ctab = keep.tile([P, 7, 7, GT], F32)
+        nc.vector.tensor_tensor(
+            out=row_part[:], in0=delta[:], in1=bt[:, 8:16].unsqueeze(1).to_broadcast([P, 7, GT]), op=ALU.mult
+        )
+        nc.vector.tensor_tensor(
+            out=row_part[:], in0=row_part[:], in1=bt[:, 0:8].unsqueeze(1).to_broadcast([P, 7, GT]), op=ALU.add
+        )
+        nc.vector.tensor_tensor(
+            out=col_part[:], in0=delta[:], in1=bt[:, 16:24].unsqueeze(1).to_broadcast([P, 7, GT]), op=ALU.mult
+        )
+        nc.vector.tensor_tensor(
+            out=ctab[:],
+            in0=row_part[:].unsqueeze(2).to_broadcast([P, 7, 7, GT]),
+            in1=col_part[:].unsqueeze(1).to_broadcast([P, 7, 7, GT]),
+            op=ALU.add,
+        )
+
+        w1g = keep.tile([P, 2, G1, 4], BF16, align_bytes=64)
+        w1w = keep.tile([P, 2 * G1], U32, align_bytes=64)
+        w1s = keep.tile([P, 2 * G1], U8, align_bytes=64)
+
+        pws = [keep.tile([P, COLS], U32, align_bytes=64, name="pw%d" % k) for k in range(NPB)]
+        pss = [keep.tile([P, COLS], U8, align_bytes=64, name="ps%d" % k) for k in range(NPB)]
+
+        def move(dst, src):
+            nc.vector.tensor_copy(out=dst.bitcast(I32), in_=src.bitcast(I32))
+
+        outv = out.rearrange("b p q e -> b (p q) e")
+
+        for s in range(CELLS):
+            a, d = divmod(s, 4)
+            if s == 0:
+                pw, psc = ow, osc
+            else:
+                pw, psc = pws[s % NPB], pss[s % NPB]
+                if s <= NPB:
+                    move(pw[0:64, :], ow[0:64, :])
+                    move(psc[0:64, :], osc[0:64, :])
+                cut = (CELLS - s) * B
+                move(pw[64:128, 0:cut], ow[64:128, COLS - cut : COLS])
+                move(pw[64:128, cut:COLS], ow[64:128, 0 : COLS - cut])
+                move(psc[64:128, 0:cut], osc[64:128, COLS - cut : COLS])
+                move(psc[64:128, cut:COLS], osc[64:128, 0 : COLS - cut])
+
+            words = []
+            for c in range(2):
+                plane = planes.tile([P, 4, COLS], BF16)
+                for t in range(4):
+                    u = 4 * c + t
+                    acc = psum1.tile([P, COLS], F32)
+                    nc.tensor.matmul_mx(
+                        out=acc[:],
+                        lhsT=w0w[:, u * P : (u + 1) * P].bitcast(FP8X4),
+                        lhsT_scale=w0s[:, u * P : (u + 1) * P],
+                        rhs=pw[:].bitcast(FP8X4),
+                        rhs_scale=psc[:],
+                        start=True,
+                        stop=True,
+                    )
+                    acc_v = acc[:].rearrange("p (r z) -> p r z", r=4)
+                    pl_v = plane[:, t, :].rearrange("p (r z) -> p r z", r=4)
+                    for dr, dc, r0, r1, c0, c1 in shift_groups(a, d):
+                        nc.scalar.activation(
+                            out=pl_v[:, r0:r1, B * c0 : B * c1],
+                            in_=acc_v[:, r0:r1, B * c0 : B * c1],
+                            func=ACT.Relu,
+                            bias=ctab[:, dr + 3, dc + 3, u : u + 1],
+                            scale=1.0,
+                        )
+                hg = grouped.tile([P, COLS, 4], BF16, align_bytes=64)
+                nc.vector.tensor_copy(
+                    out=hg[:].rearrange("p (z i) t -> p z t i", i=4),
+                    in_=plane[:].rearrange("p t (z i) -> p z t i", i=4),
+                )
+                hw = packed.tile([P, COLS], U32, align_bytes=64)
+                hs = packed.tile([P, COLS], U8, align_bytes=64)
+                nc.vector.quantize_mx(
+                    out=hw[:].bitcast(FP8X4), scales=hs[:], in_=hg[:].rearrange("p w t -> p (w t)")
+                )
+                words.append((hw, hs))
+
+            if s == 0:
+                nc.vector.tensor_copy(out=w1g[:], in_=w1raw[:].rearrange("p (c t) n -> p c n t", t=4))
+                nc.vector.quantize_mx(
+                    out=w1w[:].bitcast(FP8X4), scales=w1s[:], in_=w1g[:].rearrange("p c n t -> p (c n t)")
+                )
+
+            acc2 = psum2.tile([P, 4, G1], F32, tag="l2")
+            for r in range(4):
+                for c in range(2):
+                    hw, hs = words[c]
+                    nc.tensor.matmul_mx(
+                        out=acc2[:, r, :],
+                        lhsT=hw[:, r * P : (r + 1) * P].bitcast(FP8X4),
+                        lhsT_scale=hs[:, r * P : (r + 1) * P],
+                        rhs=w1w[:, c * G1 : (c + 1) * G1].bitcast(FP8X4),
+                        rhs_scale=w1s[:, c * G1 : (c + 1) * G1],
+                        start=(c == 0),
+                        stop=(c == 1),
+                    )
+            ot = results.tile([P, 4, G1], F32)
+            nc.vector.tensor_tensor(
+                out=ot[:], in0=acc2[:], in1=b1bc[:].unsqueeze(1).to_broadcast([P, 4, G1]), op=ALU.add
+            )
+            nc.vector.tensor_scalar_max(out=ot[:], in0=ot[:], scalar1=0.0)
+            for c in range(4):
+                split = min(4, max(0, (CELLS - s - c + 3) // 4))
+                for r0, r1, wrap in ((0, split, 0), (split, 4, -256)):
+                    if r1 <= r0:
+                        continue
+                    first = 17 * (4 * r0 + c) + 16 * s + wrap
+                    nc.sync.dma_start(
+                        out=outv[:, first : first + 68 * (r1 - r0 - 1) + 1 : 68, :],
+                        in_=ot[B * c : B * (c + 1), r0:r1, :],
+                    )

@@ -1,8 +1,6 @@
 from contextlib import ExitStack
 
-import concourse.bass as bass
 import concourse.mybir as mybir
-import concourse.tile as tile
 from concourse.masks import make_identity
 
 F32 = mybir.dt.float32
@@ -23,6 +21,8 @@ GT = G0 // P
 COLS = CELLS * B
 NPB = 3
 REL_MEAN = 0.0
+X_CELLS_ON_VECTOR = 10
+VEVAC = {}
 
 FLOPS = 2 * B * CELLS * CELLS * (512 * G0 + G0 * G1)
 
@@ -44,49 +44,72 @@ def tile_relationnetwork_pa_t_kernel(tc, x, g_W0, g_b0, g_W1, g_b1, out):
         keep = ctx.enter_context(tc.tile_pool(name="keep", bufs=1))
         planes = ctx.enter_context(tc.tile_pool(name="planes", bufs=4))
         grouped = ctx.enter_context(tc.tile_pool(name="grouped", bufs=3))
-        packed = ctx.enter_context(tc.tile_pool(name="packed", bufs=4))
+        packed = ctx.enter_context(tc.tile_pool(name="packed", bufs=6))
         results = ctx.enter_context(tc.tile_pool(name="results", bufs=3))
         psum1 = ctx.enter_context(tc.psum_pool(name="psum1", bufs=6))
         psum2 = ctx.enter_context(tc.psum_pool(name="psum2", bufs=2))
+        ctx.enter_context(tc.manual_schedule())
 
         xraw = keep.tile([P, B, 64], BF16)
-        xv = x.rearrange("b (p j) h w -> p b (j h w)", j=4)
-        nc.sync.dma_start(out=xraw[0:64], in_=xv)
-        nc.sync.dma_start(out=xraw[64:128], in_=xv)
         w0raw = keep.tile([P, 4, G0], BF16)
-        for h in range(2):
-            nc.sync.dma_start(
-                out=w0raw[:, :, h * 512 : (h + 1) * 512],
-                in_=g_W0[0:512, h * 512 : (h + 1) * 512].rearrange("(p j) g -> p j g", j=4),
-            )
         w1raw = keep.tile([P, GT, G1], BF16)
-        nc.sync.dma_start(out=w1raw[:], in_=g_W1.rearrange("(u p) n -> p u n", p=P))
-
         brow = keep.tile([P, P], BF16)
-        nc.vector.memset(brow[:], 0.0)
-        nc.scalar.dma_start(out=brow[0:8, :], in_=g_b0.rearrange("(u g) -> u g", g=P))
-        nc.scalar.dma_start(out=brow[8:24, :], in_=g_W0[512:514, :].rearrange("v (u g) -> (v u) g", g=P))
         b1bc = keep.tile([P, G1], BF16)
-        nc.scalar.dma_start(out=b1bc[:], in_=g_b1.partition_broadcast(P))
-
         ident = keep.tile([P, P], BF16)
-        make_identity(nc, ident[:])
         delta = keep.tile([P, 7, GT], F32)
-        for i in range(7):
-            nc.gpsimd.memset(delta[:, i, :], float(i - 3) - REL_MEAN)
-
-        ow = keep.tile([P, COLS], U32, align_bytes=64)
-        osc = keep.tile([P, COLS], U8, align_bytes=64)
-        nc.vector.memset(osc[:].bitcast(I32), 0)
-
+        ow2 = keep.tile([P, 2 * COLS], U32, align_bytes=64)
+        os2 = keep.tile([P, 2 * COLS], U8, align_bytes=64)
         xg = keep.tile([P, CELLS, B, 4], BF16, align_bytes=64)
-        xr = xraw[:].rearrange("p b (j n) -> p n b j", j=4)
-        nc.vector.tensor_copy(out=xg[:, 0:8], in_=xr[:, 0:8])
-        nc.scalar.copy(out=xg[:, 8:16], in_=xr[:, 8:16])
-
         w0g = keep.tile([P, G0, 4], BF16, align_bytes=64)
         w0w = keep.tile([P, G0], U32, align_bytes=64)
         w0s = keep.tile([P, G0], U8, align_bytes=64)
+        bt = keep.tile([P, 24], F32)
+        row_part = keep.tile([P, 7, GT], F32)
+        col_part = keep.tile([P, 7, GT], F32)
+        ctab = keep.tile([P, 7, 7, GT], F32)
+        w1g = keep.tile([P, 2, G1, 4], BF16, align_bytes=64)
+        w1w = keep.tile([P, 2 * G1], U32, align_bytes=64)
+        w1s = keep.tile([P, 2 * G1], U8, align_bytes=64)
+        pws = [keep.tile([P, COLS], U32, align_bytes=64, name="pw%d" % k) for k in range(NPB)]
+        pss = [keep.tile([P, COLS], U8, align_bytes=64, name="ps%d" % k) for k in range(NPB)]
+
+        nc.vector.memset(brow[:], 0.0)
+        nc.vector.memset(os2[:].bitcast(I32), 0)
+        nc.scalar.dma_start(out=brow[0:8, :], in_=g_b0.rearrange("(u g) -> u g", g=P))
+        nc.scalar.dma_start(out=brow[8:24, :], in_=g_W0[512:514, :].rearrange("v (u g) -> (v u) g", g=P))
+        xv = x.rearrange("b (p j) h w -> p b (j h w)", j=4)
+        nc.sync.dma_start(out=xraw[0:64], in_=xv)
+        nc.scalar.dma_start(out=xraw[64:128], in_=xv)
+        for h in range(4):
+            nc.sync.dma_start(
+                out=w0raw[:, :, h * 256 : (h + 1) * 256],
+                in_=g_W0[0:512, h * 256 : (h + 1) * 256].rearrange("(p j) g -> p j g", j=4),
+            )
+        nc.scalar.dma_start(out=b1bc[:], in_=g_b1.partition_broadcast(P))
+        nc.scalar.dma_start(out=w1raw[:], in_=g_W1.rearrange("(u p) n -> p u n", p=P))
+
+        make_identity(nc, ident[:])
+        for i in range(7):
+            nc.gpsimd.memset(delta[:, i, :], float(i - 3) - REL_MEAN)
+
+        bt_ps = psum2.tile([P, P], BF16, tag="l2")
+        nc.tensor.transpose(bt_ps[:], brow[:], ident[:])
+        nc.vector.tensor_copy(out=bt[:], in_=bt_ps[:, 0:24])
+        nc.vector.tensor_tensor(
+            out=row_part[:], in0=delta[:], in1=bt[:, 8:16].unsqueeze(1).to_broadcast([P, 7, GT]), op=ALU.mult
+        )
+        nc.vector.tensor_tensor(
+            out=col_part[:], in0=delta[:], in1=bt[:, 16:24].unsqueeze(1).to_broadcast([P, 7, GT]), op=ALU.mult
+        )
+        nc.vector.tensor_tensor(
+            out=row_part[:], in0=row_part[:], in1=bt[:, 0:8].unsqueeze(1).to_broadcast([P, 7, GT]), op=ALU.add
+        )
+        nc.vector.tensor_tensor(
+            out=ctab[:],
+            in0=row_part[:].unsqueeze(2).to_broadcast([P, 7, 7, GT]),
+            in1=col_part[:].unsqueeze(1).to_broadcast([P, 7, 7, GT]),
+            op=ALU.add,
+        )
 
         def w0_regroup(engine_copy, h):
             cols = slice(h * 256, (h + 1) * 256)
@@ -103,115 +126,97 @@ def tile_relationnetwork_pa_t_kernel(tc, x, g_W0, g_b0, g_W1, g_b1, out):
                 in_=w0g[:, cols, :].rearrange("p g j -> p (g j)"),
             )
 
-        w0_regroup(nc.vector.tensor_copy, 0)
-        w0_regroup(nc.scalar.copy, 1)
-        nc.vector.quantize_mx(
-            out=ow[:].bitcast(FP8X4), scales=osc[:], in_=xg[:].rearrange("p n b j -> p (n b j)")
-        )
-        w0_quantise(0)
-        w0_regroup(nc.vector.tensor_copy, 2)
-        w0_regroup(nc.scalar.copy, 3)
-        w0_quantise(1)
-        w0_quantise(2)
-        w0_quantise(3)
-
-        bt_ps = psum2.tile([P, P], BF16, tag="l2")
-        nc.tensor.transpose(bt_ps[:], brow[:], ident[:])
-        bt = keep.tile([P, 24], F32)
-        nc.vector.tensor_copy(out=bt[:], in_=bt_ps[:, 0:24])
-        row_part = keep.tile([P, 7, GT], F32)
-        col_part = keep.tile([P, 7, GT], F32)
-        ctab = keep.tile([P, 7, 7, GT], F32)
-        nc.vector.tensor_tensor(
-            out=row_part[:], in0=delta[:], in1=bt[:, 8:16].unsqueeze(1).to_broadcast([P, 7, GT]), op=ALU.mult
-        )
-        nc.vector.tensor_tensor(
-            out=row_part[:], in0=row_part[:], in1=bt[:, 0:8].unsqueeze(1).to_broadcast([P, 7, GT]), op=ALU.add
-        )
-        nc.vector.tensor_tensor(
-            out=col_part[:], in0=delta[:], in1=bt[:, 16:24].unsqueeze(1).to_broadcast([P, 7, GT]), op=ALU.mult
-        )
-        nc.vector.tensor_tensor(
-            out=ctab[:],
-            in0=row_part[:].unsqueeze(2).to_broadcast([P, 7, 7, GT]),
-            in1=col_part[:].unsqueeze(1).to_broadcast([P, 7, 7, GT]),
-            op=ALU.add,
-        )
-
-        w1g = keep.tile([P, 2, G1, 4], BF16, align_bytes=64)
-        w1w = keep.tile([P, 2 * G1], U32, align_bytes=64)
-        w1s = keep.tile([P, 2 * G1], U8, align_bytes=64)
-
-        pws = [keep.tile([P, COLS], U32, align_bytes=64, name="pw%d" % k) for k in range(NPB)]
-        pss = [keep.tile([P, COLS], U8, align_bytes=64, name="ps%d" % k) for k in range(NPB)]
-
         def move(dst, src):
             nc.vector.tensor_copy(out=dst.bitcast(I32), in_=src.bitcast(I32))
 
-        outv = out.rearrange("b p q e -> b (p q) e")
-
-        for s in range(CELLS):
-            a, d = divmod(s, 4)
+        def pair_tile(s):
             if s == 0:
-                pw, psc = ow, osc
-            else:
-                pw, psc = pws[s % NPB], pss[s % NPB]
-                if s <= NPB:
-                    move(pw[0:64, :], ow[0:64, :])
-                    move(psc[0:64, :], osc[0:64, :])
-                cut = (CELLS - s) * B
-                move(pw[64:128, 0:cut], ow[64:128, COLS - cut : COLS])
-                move(pw[64:128, cut:COLS], ow[64:128, 0 : COLS - cut])
-                move(psc[64:128, 0:cut], osc[64:128, COLS - cut : COLS])
-                move(psc[64:128, cut:COLS], osc[64:128, 0 : COLS - cut])
+                return ow2[:, 0:COLS], os2[:, 0:COLS]
+            return pws[s % NPB][:], pss[s % NPB][:]
 
-            words = []
-            for c in range(2):
-                plane = planes.tile([P, 4, COLS], BF16)
-                for t in range(4):
-                    u = 4 * c + t
-                    acc = psum1.tile([P, COLS], F32)
-                    nc.tensor.matmul_mx(
-                        out=acc[:],
-                        lhsT=w0w[:, u * P : (u + 1) * P].bitcast(FP8X4),
-                        lhsT_scale=w0s[:, u * P : (u + 1) * P],
-                        rhs=pw[:].bitcast(FP8X4),
-                        rhs_scale=psc[:],
-                        start=True,
-                        stop=True,
-                    )
-                    acc_v = acc[:].rearrange("p (r z) -> p r z", r=4)
-                    pl_v = plane[:, t, :].rearrange("p (r z) -> p r z", r=4)
-                    for dr, dc, r0, r1, c0, c1 in shift_groups(a, d):
+        def build_pair(s):
+            if s >= CELLS:
+                return
+            pw, psc = pair_tile(s)
+            if s <= NPB:
+                move(pw[0:64, :], ow2[0:64, 0:COLS])
+                move(psc[0:64, :], os2[0:64, 0:COLS])
+            move(pw[64:128, :], ow2[64:128, s * B : s * B + COLS])
+            move(psc[64:128, :], os2[64:128, s * B : s * B + COLS])
+
+        plane_of = {}
+        group_of = {}
+        words_of = {}
+        acc2_of = {}
+        ot_of = {}
+
+        def layer1(s, c):
+            a, d = divmod(s, 4)
+            pw, psc = pair_tile(s)
+            plane = planes.tile([P, 4, COLS], BF16, name="plane")
+            plane_of[(s, c)] = plane
+            for t in range(4):
+                u = 4 * c + t
+                acc = psum1.tile([P, COLS], F32, name="acc")
+                nc.tensor.matmul_mx(
+                    out=acc[:],
+                    lhsT=w0w[:, u * P : (u + 1) * P].bitcast(FP8X4),
+                    lhsT_scale=w0s[:, u * P : (u + 1) * P],
+                    rhs=pw.bitcast(FP8X4),
+                    rhs_scale=psc,
+                    start=True,
+                    stop=True,
+                )
+                acc_v = acc[:].rearrange("p (r z) -> p r z", r=4)
+                pl_v = plane[:, t, :].rearrange("p (r z) -> p r z", r=4)
+                for dr, dc, r0, r1, c0, c1 in shift_groups(a, d):
+                    bias = ctab[:, dr + 3, dc + 3, u : u + 1]
+                    if u in VEVAC.get(s, ()):
+                        nc.vector.tensor_scalar(
+                            out=pl_v[:, r0:r1, B * c0 : B * c1],
+                            in0=acc_v[:, r0:r1, B * c0 : B * c1],
+                            scalar1=bias,
+                            scalar2=0.0,
+                            op0=ALU.add,
+                            op1=ALU.max,
+                        )
+                    else:
                         nc.scalar.activation(
                             out=pl_v[:, r0:r1, B * c0 : B * c1],
                             in_=acc_v[:, r0:r1, B * c0 : B * c1],
                             func=ACT.Relu,
-                            bias=ctab[:, dr + 3, dc + 3, u : u + 1],
+                            bias=bias,
                             scale=1.0,
                         )
-                hg = grouped.tile([P, COLS, 4], BF16, align_bytes=64)
-                nc.vector.tensor_copy(
-                    out=hg[:].rearrange("p (z i) t -> p z t i", i=4),
-                    in_=plane[:].rearrange("p t (z i) -> p z t i", i=4),
-                )
-                hw = packed.tile([P, COLS], U32, align_bytes=64)
-                hs = packed.tile([P, COLS], U8, align_bytes=64)
-                nc.vector.quantize_mx(
-                    out=hw[:].bitcast(FP8X4), scales=hs[:], in_=hg[:].rearrange("p w t -> p (w t)")
-                )
-                words.append((hw, hs))
 
-            if s == 0:
-                nc.vector.tensor_copy(out=w1g[:], in_=w1raw[:].rearrange("p (c t) n -> p c n t", t=4))
-                nc.vector.quantize_mx(
-                    out=w1w[:].bitcast(FP8X4), scales=w1s[:], in_=w1g[:].rearrange("p c n t -> p (c n t)")
-                )
+        def regroup(s, c):
+            if s < 0 or s >= CELLS:
+                return
+            hg = grouped.tile([P, COLS, 4], BF16, align_bytes=64, name="hg")
+            group_of[(s, c)] = hg
+            nc.vector.tensor_copy(
+                out=hg[:].rearrange("p (z i) t -> p z t i", i=4),
+                in_=plane_of[(s, c)][:].rearrange("p t (z i) -> p z t i", i=4),
+            )
 
-            acc2 = psum2.tile([P, 4, G1], F32, tag="l2")
+        def quantise(s, c):
+            if s < 0 or s >= CELLS:
+                return
+            hw = packed.tile([P, COLS], U32, align_bytes=64, name="hw")
+            hs = packed.tile([P, COLS], U8, align_bytes=64, name="hs")
+            words_of[(s, c)] = (hw, hs)
+            nc.vector.quantize_mx(
+                out=hw[:].bitcast(FP8X4), scales=hs[:], in_=group_of[(s, c)][:].rearrange("p w t -> p (w t)")
+            )
+
+        def layer2(s):
+            if s < 0 or s >= CELLS:
+                return
+            acc2 = psum2.tile([P, 4, G1], F32, tag="l2", name="acc2")
+            acc2_of[s] = acc2
             for r in range(4):
                 for c in range(2):
-                    hw, hs = words[c]
+                    hw, hs = words_of[(s, c)]
                     nc.tensor.matmul_mx(
                         out=acc2[:, r, :],
                         lhsT=hw[:, r * P : (r + 1) * P].bitcast(FP8X4),
@@ -221,10 +226,22 @@ def tile_relationnetwork_pa_t_kernel(tc, x, g_W0, g_b0, g_W1, g_b1, out):
                         start=(c == 0),
                         stop=(c == 1),
                     )
-            ot = results.tile([P, 4, G1], F32)
+
+        def add_bias(s):
+            if s < 0 or s >= CELLS:
+                return
+            ot = results.tile([P, 4, G1], F32, name="ot")
+            ot_of[s] = ot
             nc.vector.tensor_tensor(
-                out=ot[:], in0=acc2[:], in1=b1bc[:].unsqueeze(1).to_broadcast([P, 4, G1]), op=ALU.add
+                out=ot[:], in0=acc2_of[s][:], in1=b1bc[:].unsqueeze(1).to_broadcast([P, 4, G1]), op=ALU.add
             )
+
+        outv = out.rearrange("b p q e -> b (p q) e")
+
+        def relu_store(s):
+            if s < 0 or s >= CELLS:
+                return
+            ot = ot_of[s]
             nc.vector.tensor_scalar_max(out=ot[:], in0=ot[:], scalar1=0.0)
             for c in range(4):
                 split = min(4, max(0, (CELLS - s - c + 3) // 4))
@@ -236,3 +253,41 @@ def tile_relationnetwork_pa_t_kernel(tc, x, g_W0, g_b0, g_W1, g_b1, out):
                         out=outv[:, first : first + 68 * (r1 - r0 - 1) + 1 : 68, :],
                         in_=ot[B * c : B * (c + 1), r0:r1, :],
                     )
+
+        xr = xraw[:].rearrange("p b (j n) -> p n b j", j=4)
+        nv = X_CELLS_ON_VECTOR
+        nc.vector.tensor_copy(out=xg[:, 0:nv], in_=xr[:, 0:nv])
+        nc.scalar.copy(out=xg[:, nv:CELLS], in_=xr[:, nv:CELLS])
+        w0_regroup(nc.vector.tensor_copy, 0)
+        w0_regroup(nc.scalar.copy, 1)
+        nc.vector.quantize_mx(
+            out=ow2[:, 0:COLS].bitcast(FP8X4), scales=os2[:, 0:COLS], in_=xg[:].rearrange("p n b j -> p (n b j)")
+        )
+        w0_quantise(0)
+        w0_regroup(nc.vector.tensor_copy, 2)
+        w0_quantise(1)
+        w0_regroup(nc.vector.tensor_copy, 3)
+        w0_quantise(2)
+        move(ow2[64:128, COLS : 2 * COLS], ow2[64:128, 0:COLS])
+        move(os2[64:128, COLS : 2 * COLS], os2[64:128, 0:COLS])
+        w0_quantise(3)
+        build_pair(1)
+
+        for k in range(CELLS + 3):
+            regroup(k - 1, 1)
+            add_bias(k - 3)
+            quantise(k - 1, 1)
+            relu_store(k - 3)
+            if k == 0:
+                nc.vector.tensor_copy(out=w1g[:], in_=w1raw[:].rearrange("p (c t) n -> p c n t", t=4))
+            if k < CELLS:
+                layer1(k, 0)
+                regroup(k, 0)
+                if k == 0:
+                    nc.vector.quantize_mx(
+                        out=w1w[:].bitcast(FP8X4), scales=w1s[:], in_=w1g[:].rearrange("p c n t -> p (c n t)")
+                    )
+                build_pair(k + 2)
+                quantise(k, 0)
+                layer1(k, 1)
+            layer2(k - 2)

@@ -22,7 +22,8 @@ COLS = CELLS * B
 NPB = 3
 REL_MEAN = 0.0
 X_CELLS_ON_VECTOR = 10
-VEVAC = {}
+TAIL_RELU_ON_SCALAR = 3
+VEVAC = {1: (3,), 2: (3,), 3: (3,), 5: (3,), 6: (3,), 7: (3,), 9: (3,), 10: (3,), 11: (3,), 13: (3,), 14: (3,)}
 
 FLOPS = 2 * B * CELLS * CELLS * (512 * G0 + G0 * G1)
 
@@ -242,7 +243,10 @@ def tile_relationnetwork_pa_t_kernel(tc, x, g_W0, g_b0, g_W1, g_b1, out):
             if s < 0 or s >= CELLS:
                 return
             ot = ot_of[s]
-            nc.vector.tensor_scalar_max(out=ot[:], in0=ot[:], scalar1=0.0)
+            if s >= CELLS - TAIL_RELU_ON_SCALAR:
+                nc.scalar.activation(out=ot[:], in_=ot[:], func=ACT.Relu)
+            else:
+                nc.vector.tensor_scalar_max(out=ot[:], in0=ot[:], scalar1=0.0)
             for c in range(4):
                 split = min(4, max(0, (CELLS - s - c + 3) // 4))
                 for r0, r1, wrap in ((0, split, 0), (split, 4, -256)):

@@ -19,11 +19,10 @@ G0 = 1024
 G1 = 128
 GT = G0 // P
 COLS = CELLS * B
-NPB = 3
+NPB = 4
 REL_MEAN = 0.0
 X_CELLS_ON_VECTOR = 10
-TAIL_RELU_ON_SCALAR = 3
-VEVAC = {1: (3,), 2: (3,), 3: (3,), 5: (3,), 6: (3,), 7: (3,), 9: (3,), 10: (3,), 11: (3,), 13: (3,), 14: (3,)}
+VEVAC = {}
 
 FLOPS = 2 * B * CELLS * CELLS * (512 * G0 + G0 * G1)
 
@@ -140,10 +139,10 @@ def tile_relationnetwork_pa_t_kernel(tc, x, g_W0, g_b0, g_W1, g_b1, out):
                 return
             pw, psc = pair_tile(s)
             if s <= NPB:
-                move(pw[0:64, :], ow2[0:64, 0:COLS])
-                move(psc[0:64, :], os2[0:64, 0:COLS])
-            move(pw[64:128, :], ow2[64:128, s * B : s * B + COLS])
-            move(psc[64:128, :], os2[64:128, s * B : s * B + COLS])
+                nc.sync.dma_start(out=pw[0:64, :].bitcast(I32), in_=ow2[0:64, 0:COLS].bitcast(I32))
+                nc.sync.dma_start(out=psc[0:64, :].bitcast(I32), in_=os2[0:64, 0:COLS].bitcast(I32))
+            nc.sync.dma_start(out=pw[64:128, :].bitcast(I32), in_=ow2[64:128, s * B : s * B + COLS].bitcast(I32))
+            nc.sync.dma_start(out=psc[64:128, :].bitcast(I32), in_=os2[64:128, s * B : s * B + COLS].bitcast(I32))
 
         plane_of = {}
         group_of = {}
@@ -243,10 +242,7 @@ def tile_relationnetwork_pa_t_kernel(tc, x, g_W0, g_b0, g_W1, g_b1, out):
             if s < 0 or s >= CELLS:
                 return
             ot = ot_of[s]
-            if s >= CELLS - TAIL_RELU_ON_SCALAR:
-                nc.scalar.activation(out=ot[:], in_=ot[:], func=ACT.Relu)
-            else:
-                nc.vector.tensor_scalar_max(out=ot[:], in0=ot[:], scalar1=0.0)
+            nc.vector.tensor_scalar_max(out=ot[:], in0=ot[:], scalar1=0.0)
             for c in range(4):
                 split = min(4, max(0, (CELLS - s - c + 3) // 4))
                 for r0, r1, wrap in ((0, split, 0), (split, 4, -256)):

@@ -22,7 +22,8 @@ COLS = CELLS * B
 NPB = 4
 REL_MEAN = 0.0
 X_CELLS_ON_VECTOR = 10
-VEVAC = {}
+TAIL_RELU_ON_SCALAR = 3
+VEVAC = {1: (3,), 3: (3,), 5: (3,), 6: (3,), 7: (3,), 9: (3,), 10: (3,), 11: (3,), 14: (3,)}
 
 FLOPS = 2 * B * CELLS * CELLS * (512 * G0 + G0 * G1)
 
@@ -242,7 +243,10 @@ def tile_relationnetwork_pa_t_kernel(tc, x, g_W0, g_b0, g_W1, g_b1, out):
             if s < 0 or s >= CELLS:
                 return
             ot = ot_of[s]
-            nc.vector.tensor_scalar_max(out=ot[:], in0=ot[:], scalar1=0.0)
+            if s >= CELLS - TAIL_RELU_ON_SCALAR:
+                nc.scalar.activation(out=ot[:], in_=ot[:], func=ACT.Relu)
+            else:
+                nc.vector.tensor_scalar_max(out=ot[:], in0=ot[:], scalar1=0.0)
             for c in range(4):
                 split = min(4, max(0, (CELLS - s - c + 3) // 4))
                 for r0, r1, wrap in ((0, split, 0), (split, 4, -256)):
@@ -277,7 +281,6 @@ def tile_relationnetwork_pa_t_kernel(tc, x, g_W0, g_b0, g_W1, g_b1, out):
             regroup(k - 1, 1)
             add_bias(k - 3)
             quantise(k - 1, 1)
-            relu_store(k - 3)
             if k == 0:
                 nc.vector.tensor_copy(out=w1g[:], in_=w1raw[:].rearrange("p (c t) n -> p c n t", t=4))
             if k < CELLS:
@@ -288,6 +291,8 @@ def tile_relationnetwork_pa_t_kernel(tc, x, g_W0, g_b0, g_W1, g_b1, out):
                         out=w1w[:].bitcast(FP8X4), scales=w1s[:], in_=w1g[:].rearrange("p c n t -> p (c n t)")
                     )
                 build_pair(k + 2)
+            relu_store(k - 3)
+            if k < CELLS:
                 quantise(k, 0)
                 layer1(k, 1)
             layer2(k - 2)

@@ -19,7 +19,8 @@ G0 = 1024
 G1 = 128
 GT = G0 // P
 COLS = CELLS * B
-NPB = 4
+NPB = 6
+PAIR_LEAD = 4
 REL_MEAN = 0.0
 X_CELLS_ON_VECTOR = 10
 TAIL_RELU_ON_SCALAR = 3
@@ -46,7 +47,7 @@ def tile_relationnetwork_pa_t_kernel(tc, x, g_W0, g_b0, g_W1, g_b1, out):
         planes = ctx.enter_context(tc.tile_pool(name="planes", bufs=4))
         grouped = ctx.enter_context(tc.tile_pool(name="grouped", bufs=3))
         packed = ctx.enter_context(tc.tile_pool(name="packed", bufs=6))
-        results = ctx.enter_context(tc.tile_pool(name="results", bufs=3))
+        results = ctx.enter_context(tc.tile_pool(name="results", bufs=5))
         psum1 = ctx.enter_context(tc.psum_pool(name="psum1", bufs=6))
         psum2 = ctx.enter_context(tc.psum_pool(name="psum2", bufs=2))
         ctx.enter_context(tc.manual_schedule())
@@ -86,8 +87,8 @@ def tile_relationnetwork_pa_t_kernel(tc, x, g_W0, g_b0, g_W1, g_b1, out):
                 out=w0raw[:, :, h * 256 : (h + 1) * 256],
                 in_=g_W0[0:512, h * 256 : (h + 1) * 256].rearrange("(p j) g -> p j g", j=4),
             )
-        nc.scalar.dma_start(out=b1bc[:], in_=g_b1.partition_broadcast(P))
-        nc.scalar.dma_start(out=w1raw[:], in_=g_W1.rearrange("(u p) n -> p u n", p=P))
+        nc.sync.dma_start(out=w1raw[:], in_=g_W1.rearrange("(u p) n -> p u n", p=P))
+        nc.sync.dma_start(out=b1bc[:], in_=g_b1.partition_broadcast(P))
 
         make_identity(nc, ident[:])
         for i in range(7):
@@ -275,9 +276,11 @@ def tile_relationnetwork_pa_t_kernel(tc, x, g_W0, g_b0, g_W1, g_b1, out):
         move(ow2[64:128, COLS : 2 * COLS], ow2[64:128, 0:COLS])
         move(os2[64:128, COLS : 2 * COLS], os2[64:128, 0:COLS])
         w0_quantise(3)
-        build_pair(1)
+        for s in range(1, PAIR_LEAD):
+            build_pair(s)
 
         for k in range(CELLS + 3):
+            build_pair(k + PAIR_LEAD)
             regroup(k - 1, 1)
             add_bias(k - 3)
             quantise(k - 1, 1)
@@ -290,7 +293,6 @@ def tile_relationnetwork_pa_t_kernel(tc, x, g_W0, g_b0, g_W1, g_b1, out):
                     nc.vector.quantize_mx(
                         out=w1w[:].bitcast(FP8X4), scales=w1s[:], in_=w1g[:].rearrange("p c n t -> p (c n t)")
                     )
-                build_pair(k + 2)
             relu_store(k - 3)
             if k < CELLS:
                 quantise(k, 0)

@@ -19,12 +19,11 @@ G0 = 1024
 G1 = 128
 GT = G0 // P
 COLS = CELLS * B
-NPB = 6
-PAIR_LEAD = 4
+NPB = 4
 REL_MEAN = 0.0
 X_CELLS_ON_VECTOR = 10
 TAIL_RELU_ON_SCALAR = 3
-VEVAC = {1: (3,), 3: (3,), 5: (3,), 6: (3,), 7: (3,), 9: (3,), 10: (3,), 11: (3,), 14: (3,)}
+VEVAC = {2: (3,), 5: (3,), 7: (3,), 9: (3,), 11: (3,)}
 
 FLOPS = 2 * B * CELLS * CELLS * (512 * G0 + G0 * G1)
 
@@ -47,7 +46,7 @@ def tile_relationnetwork_pa_t_kernel(tc, x, g_W0, g_b0, g_W1, g_b1, out):
         planes = ctx.enter_context(tc.tile_pool(name="planes", bufs=4))
         grouped = ctx.enter_context(tc.tile_pool(name="grouped", bufs=3))
         packed = ctx.enter_context(tc.tile_pool(name="packed", bufs=6))
-        results = ctx.enter_context(tc.tile_pool(name="results", bufs=5))
+        results = ctx.enter_context(tc.tile_pool(name="results", bufs=3))
         psum1 = ctx.enter_context(tc.psum_pool(name="psum1", bufs=6))
         psum2 = ctx.enter_context(tc.psum_pool(name="psum2", bufs=2))
         ctx.enter_context(tc.manual_schedule())
@@ -87,8 +86,8 @@ def tile_relationnetwork_pa_t_kernel(tc, x, g_W0, g_b0, g_W1, g_b1, out):
                 out=w0raw[:, :, h * 256 : (h + 1) * 256],
                 in_=g_W0[0:512, h * 256 : (h + 1) * 256].rearrange("(p j) g -> p j g", j=4),
             )
-        nc.sync.dma_start(out=w1raw[:], in_=g_W1.rearrange("(u p) n -> p u n", p=P))
-        nc.sync.dma_start(out=b1bc[:], in_=g_b1.partition_broadcast(P))
+        nc.scalar.dma_start(out=b1bc[:], in_=g_b1.partition_broadcast(P))
+        nc.scalar.dma_start(out=w1raw[:], in_=g_W1.rearrange("(u p) n -> p u n", p=P))
 
         make_identity(nc, ident[:])
         for i in range(7):
@@ -191,32 +190,40 @@ def tile_relationnetwork_pa_t_kernel(tc, x, g_W0, g_b0, g_W1, g_b1, out):
                             scale=1.0,
                         )
 
-        def regroup(s, c):
+        def regroup(s, c, lo=0, hi=COLS):
             if s < 0 or s >= CELLS:
                 return
-            hg = grouped.tile([P, COLS, 4], BF16, align_bytes=64, name="hg")
-            group_of[(s, c)] = hg
+            if lo == 0:
+                group_of[(s, c)] = grouped.tile([P, COLS, 4], BF16, align_bytes=64, name="hg")
             nc.vector.tensor_copy(
-                out=hg[:].rearrange("p (z i) t -> p z t i", i=4),
-                in_=plane_of[(s, c)][:].rearrange("p t (z i) -> p z t i", i=4),
+                out=group_of[(s, c)][:, lo:hi, :].rearrange("p (z i) t -> p z t i", i=4),
+                in_=plane_of[(s, c)][:, :, lo:hi].rearrange("p t (z i) -> p z t i", i=4),
             )
 
-        def quantise(s, c):
+        def quantise(s, c, lo=0, hi=COLS):
             if s < 0 or s >= CELLS:
                 return
-            hw = packed.tile([P, COLS], U32, align_bytes=64, name="hw")
-            hs = packed.tile([P, COLS], U8, align_bytes=64, name="hs")
-            words_of[(s, c)] = (hw, hs)
+            if lo == 0:
+                words_of[(s, c)] = (
+                    packed.tile([P, COLS], U32, align_bytes=64, name="hw"),
+                    packed.tile([P, COLS], U8, align_bytes=64, name="hs"),
+                )
+            hw, hs = words_of[(s, c)]
             nc.vector.quantize_mx(
-                out=hw[:].bitcast(FP8X4), scales=hs[:], in_=group_of[(s, c)][:].rearrange("p w t -> p (w t)")
+                out=hw[:, lo:hi].bitcast(FP8X4),
+                scales=hs[:, lo:hi],
+                in_=group_of[(s, c)][:, lo:hi, :].rearrange("p w t -> p (w t)"),
             )
 
-        def layer2(s):
+        def layer2(s, r0=0, r1=4):
             if s < 0 or s >= CELLS:
                 return
-            acc2 = psum2.tile([P, 4, G1], F32, tag="l2", name="acc2")
-            acc2_of[s] = acc2
-            for r in range(4):
+            if r1 - r0 == 4:
+                acc2 = psum2.tile([P, 4, G1], F32, tag="l2", name="acc2")
+            else:
+                acc2 = psum1.tile([P, 4, G1], F32, name="acc")
+            acc2_of[(s, r0)] = acc2
+            for r in range(r0, r1):
                 for c in range(2):
                     hw, hs = words_of[(s, c)]
                     nc.tensor.matmul_mx(
@@ -229,28 +236,32 @@ def tile_relationnetwork_pa_t_kernel(tc, x, g_W0, g_b0, g_W1, g_b1, out):
                         stop=(c == 1),
                     )
 
-        def add_bias(s):
+        def add_bias(s, r0=0, r1=4):
             if s < 0 or s >= CELLS:
                 return
-            ot = results.tile([P, 4, G1], F32, name="ot")
-            ot_of[s] = ot
+            if r0 == 0:
+                ot_of[s] = results.tile([P, 4, G1], F32, name="ot")
             nc.vector.tensor_tensor(
-                out=ot[:], in0=acc2_of[s][:], in1=b1bc[:].unsqueeze(1).to_broadcast([P, 4, G1]), op=ALU.add
+                out=ot_of[s][:, r0:r1, :],
+                in0=acc2_of[(s, r0)][:, r0:r1, :],
+                in1=b1bc[:].unsqueeze(1).to_broadcast([P, r1 - r0, G1]),
+                op=ALU.add,
             )
 
         outv = out.rearrange("b p q e -> b (p q) e")
 
-        def relu_store(s):
+        def relu_store(s, lo=0, hi=4):
             if s < 0 or s >= CELLS:
                 return
             ot = ot_of[s]
             if s >= CELLS - TAIL_RELU_ON_SCALAR:
-                nc.scalar.activation(out=ot[:], in_=ot[:], func=ACT.Relu)
+                nc.scalar.activation(out=ot[:, lo:hi, :], in_=ot[:, lo:hi, :], func=ACT.Relu)
             else:
-                nc.vector.tensor_scalar_max(out=ot[:], in0=ot[:], scalar1=0.0)
+                nc.vector.tensor_scalar_max(out=ot[:, lo:hi, :], in0=ot[:, lo:hi, :], scalar1=0.0)
             for c in range(4):
                 split = min(4, max(0, (CELLS - s - c + 3) // 4))
-                for r0, r1, wrap in ((0, split, 0), (split, 4, -256)):
+                for a0, a1, wrap in ((0, split, 0), (split, 4, -256)):
+                    r0, r1 = max(a0, lo), min(a1, hi)
                     if r1 <= r0:
                         continue
                     first = 17 * (4 * r0 + c) + 16 * s + wrap
@@ -276,25 +287,40 @@ def tile_relationnetwork_pa_t_kernel(tc, x, g_W0, g_b0, g_W1, g_b1, out):
         move(ow2[64:128, COLS : 2 * COLS], ow2[64:128, 0:COLS])
         move(os2[64:128, COLS : 2 * COLS], os2[64:128, 0:COLS])
         w0_quantise(3)
-        for s in range(1, PAIR_LEAD):
-            build_pair(s)
+        build_pair(1)
 
-        for k in range(CELLS + 3):
-            build_pair(k + PAIR_LEAD)
+        for k in range(CELLS):
             regroup(k - 1, 1)
             add_bias(k - 3)
             quantise(k - 1, 1)
             if k == 0:
                 nc.vector.tensor_copy(out=w1g[:], in_=w1raw[:].rearrange("p (c t) n -> p c n t", t=4))
-            if k < CELLS:
-                layer1(k, 0)
-                regroup(k, 0)
-                if k == 0:
-                    nc.vector.quantize_mx(
-                        out=w1w[:].bitcast(FP8X4), scales=w1s[:], in_=w1g[:].rearrange("p c n t -> p (c n t)")
-                    )
+            layer1(k, 0)
+            regroup(k, 0)
+            if k == 0:
+                nc.vector.quantize_mx(
+                    out=w1w[:].bitcast(FP8X4), scales=w1s[:], in_=w1g[:].rearrange("p c n t -> p (c n t)")
+                )
+            build_pair(k + 2)
             relu_store(k - 3)
-            if k < CELLS:
-                quantise(k, 0)
-                layer1(k, 1)
+            quantise(k, 0)
+            layer1(k, 1)
             layer2(k - 2)
+
+        last = CELLS - 1
+        half = COLS // 2
+        add_bias(last - 2)
+        regroup(last, 1, 0, half)
+        regroup(last, 1, half, COLS)
+        quantise(last, 1, 0, half)
+        quantise(last, 1, half, COLS)
+        relu_store(last - 2)
+        layer2(last - 1)
+        add_bias(last - 1)
+        relu_store(last - 1)
+        layer2(last, 0, 2)
+        layer2(last, 2, 4)
+        add_bias(last, 0, 2)
+        relu_store(last, 0, 2)
+        add_bias(last, 2, 4)
+        relu_store(last, 2, 4)

@@ -51,6 +51,7 @@ def tile_relationnetwork_pa_t_kernel(tc, x, g_W0, g_b0, g_W1, g_b1, out):
         psum2 = ctx.enter_context(tc.psum_pool(name="psum2", bufs=2))
         ctx.enter_context(tc.manual_schedule())
 
+        warm = keep.tile([P, 8], F32)
         xraw = keep.tile([P, B, 64], BF16)
         w0raw = keep.tile([P, 4, G0], BF16)
         w1raw = keep.tile([P, GT, G1], BF16)
@@ -76,18 +77,20 @@ def tile_relationnetwork_pa_t_kernel(tc, x, g_W0, g_b0, g_W1, g_b1, out):
 
         nc.vector.memset(brow[:], 0.0)
         nc.vector.memset(os2[:].bitcast(I32), 0)
-        nc.scalar.dma_start(out=brow[0:8, :], in_=g_b0.rearrange("(u g) -> u g", g=P))
-        nc.scalar.dma_start(out=brow[8:24, :], in_=g_W0[512:514, :].rearrange("v (u g) -> (v u) g", g=P))
+        nc.gpsimd.memset(warm[:], 0.0)
         xv = x.rearrange("b (p j) h w -> p b (j h w)", j=4)
         nc.sync.dma_start(out=xraw[0:64], in_=xv)
         nc.scalar.dma_start(out=xraw[64:128], in_=xv)
+        nc.scalar.dma_start(out=brow[0:8, :], in_=g_b0.rearrange("(u g) -> u g", g=P))
+        nc.scalar.dma_start(out=brow[8:24, :], in_=g_W0[512:514, :].rearrange("v (u g) -> (v u) g", g=P))
+        nc.scalar.activation(out=warm[:], in_=warm[:], func=ACT.Relu)
         for h in range(4):
             nc.sync.dma_start(
                 out=w0raw[:, :, h * 256 : (h + 1) * 256],
                 in_=g_W0[0:512, h * 256 : (h + 1) * 256].rearrange("(p j) g -> p j g", j=4),
             )
-        nc.scalar.dma_start(out=b1bc[:], in_=g_b1.partition_broadcast(P))
-        nc.scalar.dma_start(out=w1raw[:], in_=g_W1.rearrange("(u p) n -> p u n", p=P))
+        nc.sync.dma_start(out=w1raw[:], in_=g_W1.rearrange("(u p) n -> p u n", p=P))
+        nc.sync.dma_start(out=b1bc[:], in_=g_b1.partition_broadcast(P))
 
         make_identity(nc, ident[:])
         for i in range(7):
@@ -95,22 +98,23 @@ def tile_relationnetwork_pa_t_kernel(tc, x, g_W0, g_b0, g_W1, g_b1, out):
 
         bt_ps = psum2.tile([P, P], BF16, tag="l2")
         nc.tensor.transpose(bt_ps[:], brow[:], ident[:])
-        nc.vector.tensor_copy(out=bt[:], in_=bt_ps[:, 0:24])
-        nc.vector.tensor_tensor(
-            out=row_part[:], in0=delta[:], in1=bt[:, 8:16].unsqueeze(1).to_broadcast([P, 7, GT]), op=ALU.mult
-        )
-        nc.vector.tensor_tensor(
-            out=col_part[:], in0=delta[:], in1=bt[:, 16:24].unsqueeze(1).to_broadcast([P, 7, GT]), op=ALU.mult
-        )
-        nc.vector.tensor_tensor(
-            out=row_part[:], in0=row_part[:], in1=bt[:, 0:8].unsqueeze(1).to_broadcast([P, 7, GT]), op=ALU.add
-        )
-        nc.vector.tensor_tensor(
-            out=ctab[:],
-            in0=row_part[:].unsqueeze(2).to_broadcast([P, 7, 7, GT]),
-            in1=col_part[:].unsqueeze(1).to_broadcast([P, 7, 7, GT]),
-            op=ALU.add,
-        )
+
+        def bias_table():
+            nc.vector.tensor_tensor(
+                out=row_part[:], in0=delta[:], in1=bt[:, 8:16].unsqueeze(1).to_broadcast([P, 7, GT]), op=ALU.mult
+            )
+            nc.vector.tensor_tensor(
+                out=col_part[:], in0=delta[:], in1=bt[:, 16:24].unsqueeze(1).to_broadcast([P, 7, GT]), op=ALU.mult
+            )
+            nc.vector.tensor_tensor(
+                out=row_part[:], in0=row_part[:], in1=bt[:, 0:8].unsqueeze(1).to_broadcast([P, 7, GT]), op=ALU.add
+            )
+            nc.vector.tensor_tensor(
+                out=ctab[:],
+                in0=row_part[:].unsqueeze(2).to_broadcast([P, 7, 7, GT]),
+                in1=col_part[:].unsqueeze(1).to_broadcast([P, 7, 7, GT]),
+                op=ALU.add,
+            )
 
         def w0_regroup(engine_copy, h):
             cols = slice(h * 256, (h + 1) * 256)
@@ -171,7 +175,7 @@ def tile_relationnetwork_pa_t_kernel(tc, x, g_W0, g_b0, g_W1, g_b1, out):
                 acc_v = acc[:].rearrange("p (r z) -> p r z", r=4)
                 pl_v = plane[:, t, :].rearrange("p (r z) -> p r z", r=4)
                 for dr, dc, r0, r1, c0, c1 in shift_groups(a, d):
-                    bias = ctab[:, dr + 3, dc + 3, u : u + 1]
+                    bias = bt[:, u : u + 1] if s == 0 else ctab[:, dr + 3, dc + 3, u : u + 1]
                     if u in VEVAC.get(s, ()):
                         nc.vector.tensor_scalar(
                             out=pl_v[:, r0:r1, B * c0 : B * c1],
@@ -280,14 +284,16 @@ def tile_relationnetwork_pa_t_kernel(tc, x, g_W0, g_b0, g_W1, g_b1, out):
             out=ow2[:, 0:COLS].bitcast(FP8X4), scales=os2[:, 0:COLS], in_=xg[:].rearrange("p n b j -> p (n b j)")
         )
         w0_quantise(0)
-        w0_regroup(nc.vector.tensor_copy, 2)
+        nc.vector.tensor_copy(out=bt[:], in_=bt_ps[:, 0:24])
         w0_quantise(1)
-        w0_regroup(nc.vector.tensor_copy, 3)
-        w0_quantise(2)
         move(ow2[64:128, COLS : 2 * COLS], ow2[64:128, 0:COLS])
         move(os2[64:128, COLS : 2 * COLS], os2[64:128, 0:COLS])
+        w0_regroup(nc.vector.tensor_copy, 2)
+        w0_regroup(nc.vector.tensor_copy, 3)
+        w0_quantise(2)
         w0_quantise(3)
         build_pair(1)
+        bias_table()
 
         for k in range(CELLS):
             regroup(k - 1, 1)

@@ -22,8 +22,8 @@ COLS = CELLS * B
 NPB = 4
 REL_MEAN = 0.0
 X_CELLS_ON_VECTOR = 10
-TAIL_RELU_ON_SCALAR = 3
-VEVAC = {2: (3,), 5: (3,), 7: (3,), 9: (3,), 11: (3,)}
+ORDER = [s for s in range(CELLS) if s != 8] + [8]
+VECTOR_ROW = {2: 3, 4: 3, 6: 3, 10: 0, 12: 0, 14: 0}
 
 FLOPS = 2 * B * CELLS * CELLS * (512 * G0 + G0 * G1)
 
@@ -44,11 +44,12 @@ def tile_relationnetwork_pa_t_kernel(tc, x, g_W0, g_b0, g_W1, g_b1, out):
     with ExitStack() as ctx:
         keep = ctx.enter_context(tc.tile_pool(name="keep", bufs=1))
         planes = ctx.enter_context(tc.tile_pool(name="planes", bufs=4))
-        grouped = ctx.enter_context(tc.tile_pool(name="grouped", bufs=3))
+        grouped = ctx.enter_context(tc.tile_pool(name="grouped", bufs=4))
         packed = ctx.enter_context(tc.tile_pool(name="packed", bufs=6))
         results = ctx.enter_context(tc.tile_pool(name="results", bufs=3))
         psum1 = ctx.enter_context(tc.psum_pool(name="psum1", bufs=6))
-        psum2 = ctx.enter_context(tc.psum_pool(name="psum2", bufs=2))
+        psumv = ctx.enter_context(tc.psum_pool(name="psumv", bufs=1))
+        psum2 = ctx.enter_context(tc.psum_pool(name="psum2", bufs=1))
         ctx.enter_context(tc.manual_schedule())
 
         warm = keep.tile([P, 8], F32)
@@ -96,7 +97,7 @@ def tile_relationnetwork_pa_t_kernel(tc, x, g_W0, g_b0, g_W1, g_b1, out):
         for i in range(7):
             nc.gpsimd.memset(delta[:, i, :], float(i - 3) - REL_MEAN)
 
-        bt_ps = psum2.tile([P, P], BF16, tag="l2")
+        bt_ps = psumv.tile([P, P], BF16, name="vacc")
         nc.tensor.transpose(bt_ps[:], brow[:], ident[:])
 
         def bias_table():
@@ -134,16 +135,17 @@ def tile_relationnetwork_pa_t_kernel(tc, x, g_W0, g_b0, g_W1, g_b1, out):
         def move(dst, src):
             nc.vector.tensor_copy(out=dst.bitcast(I32), in_=src.bitcast(I32))
 
-        def pair_tile(s):
-            if s == 0:
+        def pair_tile(k):
+            if k == 0:
                 return ow2[:, 0:COLS], os2[:, 0:COLS]
-            return pws[s % NPB][:], pss[s % NPB][:]
+            return pws[k % NPB][:], pss[k % NPB][:]
 
-        def build_pair(s):
-            if s >= CELLS:
+        def build_pair(k):
+            if k >= CELLS:
                 return
-            pw, psc = pair_tile(s)
-            if s <= NPB:
+            s = ORDER[k]
+            pw, psc = pair_tile(k)
+            if k <= NPB:
                 nc.sync.dma_start(out=pw[0:64, :].bitcast(I32), in_=ow2[0:64, 0:COLS].bitcast(I32))
                 nc.sync.dma_start(out=psc[0:64, :].bitcast(I32), in_=os2[0:64, 0:COLS].bitcast(I32))
             nc.sync.dma_start(out=pw[64:128, :].bitcast(I32), in_=ow2[64:128, s * B : s * B + COLS].bitcast(I32))
@@ -154,15 +156,74 @@ def tile_relationnetwork_pa_t_kernel(tc, x, g_W0, g_b0, g_W1, g_b1, out):
         words_of = {}
         acc2_of = {}
         ot_of = {}
+        rowacc_of = {}
 
-        def layer1(s, c):
-            a, d = divmod(s, 4)
-            pw, psc = pair_tile(s)
-            plane = planes.tile([P, 4, COLS], BF16, name="plane")
-            plane_of[(s, c)] = plane
+        def scalar_rows(k):
+            v = VECTOR_ROW.get(ORDER[k])
+            return (1, 4) if v == 0 else (0, 3) if v == 3 else (0, 4)
+
+        def new_group(k, c):
+            if (k, c) not in group_of:
+                group_of[(k, c)] = grouped.tile([P, COLS, 4], BF16, align_bytes=64, name="hg")
+            return group_of[(k, c)]
+
+        def row_matmul(k, c):
+            if k >= CELLS or ORDER[k] not in VECTOR_ROW:
+                return
+            v = VECTOR_ROW[ORDER[k]]
+            pw, psc = pair_tile(k)
+            acc = psumv.tile([P, COLS], F32, name="vacc")
+            rowacc_of[(k, c)] = acc
             for t in range(4):
                 u = 4 * c + t
+                nc.tensor.matmul_mx(
+                    out=acc[:, t * P : (t + 1) * P],
+                    lhsT=w0w[:, u * P : (u + 1) * P].bitcast(FP8X4),
+                    lhsT_scale=w0s[:, u * P : (u + 1) * P],
+                    rhs=pw[:, v * P : (v + 1) * P].bitcast(FP8X4),
+                    rhs_scale=psc[:, v * P : (v + 1) * P],
+                    start=True,
+                    stop=True,
+                )
+
+        def row_add(k, c):
+            if k >= CELLS or ORDER[k] not in VECTOR_ROW:
+                return
+            s = ORDER[k]
+            v = VECTOR_ROW[s]
+            a, d = divmod(s, 4)
+            acc_v = rowacc_of[(k, c)][:].rearrange("p (t n) -> p n t", t=4)
+            hg = new_group(k, c)
+            for dr, dc, r0, r1, c0, c1 in shift_groups(a, d):
+                if not r0 <= v < r1:
+                    continue
+                nc.vector.tensor_tensor(
+                    out=hg[:, v * P + B * c0 : v * P + B * c1, :],
+                    in0=acc_v[:, B * c0 : B * c1, :],
+                    in1=ctab[:, dr + 3, dc + 3, 4 * c : 4 * c + 4].unsqueeze(1).to_broadcast([P, B * (c1 - c0), 4]),
+                    op=ALU.add,
+                )
+
+        def row_relu(k, c):
+            if k < 0 or k >= CELLS or ORDER[k] not in VECTOR_ROW:
+                return
+            v = VECTOR_ROW[ORDER[k]]
+            hg = group_of[(k, c)][:, v * P : (v + 1) * P, :].rearrange("p n t -> p (n t)")
+            nc.vector.tensor_scalar_max(out=hg, in0=hg, scalar1=0.0)
+
+        def layer1(k, c, halves=1):
+            s = ORDER[k]
+            a, d = divmod(s, 4)
+            pw, psc = pair_tile(k)
+            plane = planes.tile([P, 4, COLS], BF16, name="plane")
+            plane_of[(k, c)] = plane
+            lo, hi = scalar_rows(k)
+            accs = []
+
+            def multiply(t):
+                u = 4 * c + t
                 acc = psum1.tile([P, COLS], F32, name="acc")
+                accs.append(acc)
                 nc.tensor.matmul_mx(
                     out=acc[:],
                     lhsT=w0w[:, u * P : (u + 1) * P].bitcast(FP8X4),
@@ -172,64 +233,70 @@ def tile_relationnetwork_pa_t_kernel(tc, x, g_W0, g_b0, g_W1, g_b1, out):
                     start=True,
                     stop=True,
                 )
-                acc_v = acc[:].rearrange("p (r z) -> p r z", r=4)
+
+            def empty(t, lo, hi):
+                u = 4 * c + t
+                acc_v = accs[t][:].rearrange("p (r z) -> p r z", r=4)
                 pl_v = plane[:, t, :].rearrange("p (r z) -> p r z", r=4)
                 for dr, dc, r0, r1, c0, c1 in shift_groups(a, d):
+                    r0, r1 = max(r0, lo), min(r1, hi)
+                    if r1 <= r0:
+                        continue
                     bias = bt[:, u : u + 1] if s == 0 else ctab[:, dr + 3, dc + 3, u : u + 1]
-                    if u in VEVAC.get(s, ()):
-                        nc.vector.tensor_scalar(
-                            out=pl_v[:, r0:r1, B * c0 : B * c1],
-                            in0=acc_v[:, r0:r1, B * c0 : B * c1],
-                            scalar1=bias,
-                            scalar2=0.0,
-                            op0=ALU.add,
-                            op1=ALU.max,
-                        )
-                    else:
-                        nc.scalar.activation(
-                            out=pl_v[:, r0:r1, B * c0 : B * c1],
-                            in_=acc_v[:, r0:r1, B * c0 : B * c1],
-                            func=ACT.Relu,
-                            bias=bias,
-                            scale=1.0,
-                        )
+                    nc.scalar.activation(
+                        out=pl_v[:, r0:r1, B * c0 : B * c1],
+                        in_=acc_v[:, r0:r1, B * c0 : B * c1],
+                        func=ACT.Relu,
+                        bias=bias,
+                        scale=1.0,
+                    )
 
-        def regroup(s, c, lo=0, hi=COLS):
-            if s < 0 or s >= CELLS:
+            for t in range(4):
+                multiply(t)
+                if halves == 1:
+                    empty(t, lo, hi)
+            if halves == 2:
+                for h in range(2):
+                    for t in range(4):
+                        empty(t, 2 * h, 2 * h + 2)
+
+        def regroup(k, c, lo=None, hi=None):
+            if k < 0 or k >= CELLS:
                 return
-            if lo == 0:
-                group_of[(s, c)] = grouped.tile([P, COLS, 4], BF16, align_bytes=64, name="hg")
+            if lo is None:
+                r0, r1 = scalar_rows(k)
+                lo, hi = r0 * P, r1 * P
             nc.vector.tensor_copy(
-                out=group_of[(s, c)][:, lo:hi, :].rearrange("p (z i) t -> p z t i", i=4),
-                in_=plane_of[(s, c)][:, :, lo:hi].rearrange("p t (z i) -> p z t i", i=4),
+                out=new_group(k, c)[:, lo:hi, :].rearrange("p (z i) t -> p z t i", i=4),
+                in_=plane_of[(k, c)][:, :, lo:hi].rearrange("p t (z i) -> p z t i", i=4),
             )
 
-        def quantise(s, c, lo=0, hi=COLS):
-            if s < 0 or s >= CELLS:
+        def quantise(k, c, lo=0, hi=COLS):
+            if k < 0 or k >= CELLS:
                 return
             if lo == 0:
-                words_of[(s, c)] = (
+                words_of[(k, c)] = (
                     packed.tile([P, COLS], U32, align_bytes=64, name="hw"),
                     packed.tile([P, COLS], U8, align_bytes=64, name="hs"),
                 )
-            hw, hs = words_of[(s, c)]
+            hw, hs = words_of[(k, c)]
             nc.vector.quantize_mx(
                 out=hw[:, lo:hi].bitcast(FP8X4),
                 scales=hs[:, lo:hi],
-                in_=group_of[(s, c)][:, lo:hi, :].rearrange("p w t -> p (w t)"),
+                in_=group_of[(k, c)][:, lo:hi, :].rearrange("p w t -> p (w t)"),
             )
 
-        def layer2(s, r0=0, r1=4):
-            if s < 0 or s >= CELLS:
+        def layer2(k, r0=0, r1=4):
+            if k < 0 or k >= CELLS:
                 return
-            if r1 - r0 == 4:
+            if r1 - r0 == 4 and k < CELLS - 2:
                 acc2 = psum2.tile([P, 4, G1], F32, tag="l2", name="acc2")
             else:
                 acc2 = psum1.tile([P, 4, G1], F32, name="acc")
-            acc2_of[(s, r0)] = acc2
+            acc2_of[(k, r0)] = acc2
             for r in range(r0, r1):
                 for c in range(2):
-                    hw, hs = words_of[(s, c)]
+                    hw, hs = words_of[(k, c)]
                     nc.tensor.matmul_mx(
                         out=acc2[:, r, :],
                         lhsT=hw[:, r * P : (r + 1) * P].bitcast(FP8X4),
@@ -240,25 +307,26 @@ def tile_relationnetwork_pa_t_kernel(tc, x, g_W0, g_b0, g_W1, g_b1, out):
                         stop=(c == 1),
                     )
 
-        def add_bias(s, r0=0, r1=4):
-            if s < 0 or s >= CELLS:
+        def add_bias(k, r0=0, r1=4):
+            if k < 0 or k >= CELLS:
                 return
             if r0 == 0:
-                ot_of[s] = results.tile([P, 4, G1], F32, name="ot")
+                ot_of[k] = results.tile([P, 4, G1], F32, name="ot")
             nc.vector.tensor_tensor(
-                out=ot_of[s][:, r0:r1, :],
-                in0=acc2_of[(s, r0)][:, r0:r1, :],
+                out=ot_of[k][:, r0:r1, :],
+                in0=acc2_of[(k, r0)][:, r0:r1, :],
                 in1=b1bc[:].unsqueeze(1).to_broadcast([P, r1 - r0, G1]),
                 op=ALU.add,
             )
 
         outv = out.rearrange("b p q e -> b (p q) e")
 
-        def relu_store(s, lo=0, hi=4):
-            if s < 0 or s >= CELLS:
+        def relu_store(k, lo=0, hi=4):
+            if k < 0 or k >= CELLS:
                 return
-            ot = ot_of[s]
-            if s >= CELLS - TAIL_RELU_ON_SCALAR:
+            s = ORDER[k]
+            ot = ot_of[k]
+            if k >= CELLS - 2:
                 nc.scalar.activation(out=ot[:, lo:hi, :], in_=ot[:, lo:hi, :], func=ACT.Relu)
             else:
                 nc.vector.tensor_scalar_max(out=ot[:, lo:hi, :], in0=ot[:, lo:hi, :], scalar1=0.0)
@@ -295,10 +363,14 @@ def tile_relationnetwork_pa_t_kernel(tc, x, g_W0, g_b0, g_W1, g_b1, out):
         build_pair(1)
         bias_table()
 
+        last = CELLS - 1
         for k in range(CELLS):
             regroup(k - 1, 1)
+            row_relu(k - 1, 1)
             add_bias(k - 3)
             quantise(k - 1, 1)
+            row_matmul(k, 0)
+            row_add(k, 0)
             if k == 0:
                 nc.vector.tensor_copy(out=w1g[:], in_=w1raw[:].rearrange("p (c t) n -> p c n t", t=4))
             layer1(k, 0)
@@ -307,26 +379,28 @@ def tile_relationnetwork_pa_t_kernel(tc, x, g_W0, g_b0, g_W1, g_b1, out):
                 nc.vector.quantize_mx(
                     out=w1w[:].bitcast(FP8X4), scales=w1s[:], in_=w1g[:].rearrange("p c n t -> p (c n t)")
                 )
+            row_relu(k, 0)
             build_pair(k + 2)
             relu_store(k - 3)
             quantise(k, 0)
-            layer1(k, 1)
+            layer1(k, 1, 2 if k == last else 1)
+            row_matmul(k, 1)
+            row_add(k, 1)
             layer2(k - 2)
 
-        last = CELLS - 1
         half = COLS // 2
         add_bias(last - 2)
-        regroup(last, 1, 0, half)
-        regroup(last, 1, half, COLS)
-        quantise(last, 1, 0, half)
-        quantise(last, 1, half, COLS)
-        relu_store(last - 2)
         layer2(last - 1)
+        regroup(last, 1, 0, half)
+        relu_store(last - 2)
         add_bias(last - 1)
+        quantise(last, 1, 0, half)
         relu_store(last - 1)
+        regroup(last, 1, half, COLS)
         layer2(last, 0, 2)
-        layer2(last, 2, 4)
+        quantise(last, 1, half, COLS)
         add_bias(last, 0, 2)
         relu_store(last, 0, 2)
+        layer2(last, 2, 4)
         add_bias(last, 2, 4)
         relu_store(last, 2, 4)

@@ -23,7 +23,6 @@ NPB = 4
 REL_MEAN = 0.0
 X_CELLS_ON_VECTOR = 10
 ORDER = [s for s in range(CELLS) if s != 8] + [8]
-VECTOR_ROW = {2: 3, 4: 3, 6: 3, 10: 0, 12: 0, 14: 0}
 
 FLOPS = 2 * B * CELLS * CELLS * (512 * G0 + G0 * G1)
 
@@ -44,12 +43,11 @@ def tile_relationnetwork_pa_t_kernel(tc, x, g_W0, g_b0, g_W1, g_b1, out):
     with ExitStack() as ctx:
         keep = ctx.enter_context(tc.tile_pool(name="keep", bufs=1))
         planes = ctx.enter_context(tc.tile_pool(name="planes", bufs=4))
-        grouped = ctx.enter_context(tc.tile_pool(name="grouped", bufs=4))
+        grouped = ctx.enter_context(tc.tile_pool(name="grouped", bufs=3))
         packed = ctx.enter_context(tc.tile_pool(name="packed", bufs=6))
         results = ctx.enter_context(tc.tile_pool(name="results", bufs=3))
         psum1 = ctx.enter_context(tc.psum_pool(name="psum1", bufs=6))
-        psumv = ctx.enter_context(tc.psum_pool(name="psumv", bufs=1))
-        psum2 = ctx.enter_context(tc.psum_pool(name="psum2", bufs=1))
+        psum2 = ctx.enter_context(tc.psum_pool(name="psum2", bufs=2))
         ctx.enter_context(tc.manual_schedule())
 
         warm = keep.tile([P, 8], F32)
@@ -97,7 +95,7 @@ def tile_relationnetwork_pa_t_kernel(tc, x, g_W0, g_b0, g_W1, g_b1, out):
         for i in range(7):
             nc.gpsimd.memset(delta[:, i, :], float(i - 3) - REL_MEAN)
 
-        bt_ps = psumv.tile([P, P], BF16, name="vacc")
+        bt_ps = psum2.tile([P, P], BF16, tag="l2")
         nc.tensor.transpose(bt_ps[:], brow[:], ident[:])
 
         def bias_table():
@@ -156,60 +154,11 @@ def tile_relationnetwork_pa_t_kernel(tc, x, g_W0, g_b0, g_W1, g_b1, out):
         words_of = {}
         acc2_of = {}
         ot_of = {}
-        rowacc_of = {}
-
-        def scalar_rows(k):
-            v = VECTOR_ROW.get(ORDER[k])
-            return (1, 4) if v == 0 else (0, 3) if v == 3 else (0, 4)
 
         def new_group(k, c):
             if (k, c) not in group_of:
                 group_of[(k, c)] = grouped.tile([P, COLS, 4], BF16, align_bytes=64, name="hg")
             return group_of[(k, c)]
-
-        def row_matmul(k, c):
-            if k >= CELLS or ORDER[k] not in VECTOR_ROW:
-                return
-            v = VECTOR_ROW[ORDER[k]]
-            pw, psc = pair_tile(k)
-            acc = psumv.tile([P, COLS], F32, name="vacc")
-            rowacc_of[(k, c)] = acc
-            for t in range(4):
-                u = 4 * c + t
-                nc.tensor.matmul_mx(
-                    out=acc[:, t * P : (t + 1) * P],
-                    lhsT=w0w[:, u * P : (u + 1) * P].bitcast(FP8X4),
-                    lhsT_scale=w0s[:, u * P : (u + 1) * P],
-                    rhs=pw[:, v * P : (v + 1) * P].bitcast(FP8X4),
-                    rhs_scale=psc[:, v * P : (v + 1) * P],
-                    start=True,
-                    stop=True,
-                )
-
-        def row_add(k, c):
-            if k >= CELLS or ORDER[k] not in VECTOR_ROW:
-                return
-            s = ORDER[k]
-            v = VECTOR_ROW[s]
-            a, d = divmod(s, 4)
-            acc_v = rowacc_of[(k, c)][:].rearrange("p (t n) -> p n t", t=4)
-            hg = new_group(k, c)
-            for dr, dc, r0, r1, c0, c1 in shift_groups(a, d):
-                if not r0 <= v < r1:
-                    continue
-                nc.vector.tensor_tensor(
-                    out=hg[:, v * P + B * c0 : v * P + B * c1, :],
-                    in0=acc_v[:, B * c0 : B * c1, :],
-                    in1=ctab[:, dr + 3, dc + 3, 4 * c : 4 * c + 4].unsqueeze(1).to_broadcast([P, B * (c1 - c0), 4]),
-                    op=ALU.add,
-                )
-
-        def row_relu(k, c):
-            if k < 0 or k >= CELLS or ORDER[k] not in VECTOR_ROW:
-                return
-            v = VECTOR_ROW[ORDER[k]]
-            hg = group_of[(k, c)][:, v * P : (v + 1) * P, :].rearrange("p n t -> p (n t)")
-            nc.vector.tensor_scalar_max(out=hg, in0=hg, scalar1=0.0)
 
         def layer1(k, c, halves=1):
             s = ORDER[k]
@@ -217,7 +166,6 @@ def tile_relationnetwork_pa_t_kernel(tc, x, g_W0, g_b0, g_W1, g_b1, out):
             pw, psc = pair_tile(k)
             plane = planes.tile([P, 4, COLS], BF16, name="plane")
             plane_of[(k, c)] = plane
-            lo, hi = scalar_rows(k)
             accs = []
 
             def multiply(t):
@@ -254,18 +202,15 @@ def tile_relationnetwork_pa_t_kernel(tc, x, g_W0, g_b0, g_W1, g_b1, out):
             for t in range(4):
                 multiply(t)
                 if halves == 1:
-                    empty(t, lo, hi)
+                    empty(t, 0, 4)
             if halves == 2:
                 for h in range(2):
                     for t in range(4):
                         empty(t, 2 * h, 2 * h + 2)
 
-        def regroup(k, c, lo=None, hi=None):
+        def regroup(k, c, lo=0, hi=COLS):
             if k < 0 or k >= CELLS:
                 return
-            if lo is None:
-                r0, r1 = scalar_rows(k)
-                lo, hi = r0 * P, r1 * P
             nc.vector.tensor_copy(
                 out=new_group(k, c)[:, lo:hi, :].rearrange("p (z i) t -> p z t i", i=4),
                 in_=plane_of[(k, c)][:, :, lo:hi].rearrange("p t (z i) -> p z t i", i=4),
@@ -366,11 +311,8 @@ def tile_relationnetwork_pa_t_kernel(tc, x, g_W0, g_b0, g_W1, g_b1, out):
         last = CELLS - 1
         for k in range(CELLS):
             regroup(k - 1, 1)
-            row_relu(k - 1, 1)
             add_bias(k - 3)
             quantise(k - 1, 1)
-            row_matmul(k, 0)
-            row_add(k, 0)
             if k == 0:
                 nc.vector.tensor_copy(out=w1g[:], in_=w1raw[:].rearrange("p (c t) n -> p c n t", t=4))
             layer1(k, 0)
@@ -379,13 +321,10 @@ def tile_relationnetwork_pa_t_kernel(tc, x, g_W0, g_b0, g_W1, g_b1, out):
                 nc.vector.quantize_mx(
                     out=w1w[:].bitcast(FP8X4), scales=w1s[:], in_=w1g[:].rearrange("p c n t -> p (c n t)")
                 )
-            row_relu(k, 0)
             build_pair(k + 2)
             relu_store(k - 3)
             quantise(k, 0)
             layer1(k, 1, 2 if k == last else 1)
-            row_matmul(k, 1)
-            row_add(k, 1)
             layer2(k - 2)
 
         half = COLS // 2

@@ -22,6 +22,7 @@ COLS = CELLS * B
 NPB = 4
 REL_MEAN = 0.0
 X_CELLS_ON_VECTOR = 10
+PAIR_SWAP = (1, 0, 3, 2)
 ORDER = [s for s in range(CELLS) if s != 8] + [8]
 
 FLOPS = 2 * B * CELLS * CELLS * (512 * G0 + G0 * G1)
@@ -42,10 +43,10 @@ def tile_relationnetwork_pa_t_kernel(tc, x, g_W0, g_b0, g_W1, g_b1, out):
     nc = tc.nc
     with ExitStack() as ctx:
         keep = ctx.enter_context(tc.tile_pool(name="keep", bufs=1))
-        planes = ctx.enter_context(tc.tile_pool(name="planes", bufs=4))
+        planes = ctx.enter_context(tc.tile_pool(name="planes", bufs=6))
         grouped = ctx.enter_context(tc.tile_pool(name="grouped", bufs=3))
         packed = ctx.enter_context(tc.tile_pool(name="packed", bufs=6))
-        results = ctx.enter_context(tc.tile_pool(name="results", bufs=3))
+        results = ctx.enter_context(tc.tile_pool(name="results", bufs=CELLS))
         psum1 = ctx.enter_context(tc.psum_pool(name="psum1", bufs=6))
         psum2 = ctx.enter_context(tc.psum_pool(name="psum2", bufs=2))
         ctx.enter_context(tc.manual_schedule())
@@ -201,12 +202,12 @@ def tile_relationnetwork_pa_t_kernel(tc, x, g_W0, g_b0, g_W1, g_b1, out):
 
             for t in range(4):
                 multiply(t)
-                if halves == 1:
+                if k == 0:
                     empty(t, 0, 4)
-            if halves == 2:
-                for h in range(2):
-                    for t in range(4):
-                        empty(t, 2 * h, 2 * h + 2)
+            if k > 0:
+                for h in range(halves):
+                    for t in PAIR_SWAP:
+                        empty(t, 4 // halves * h, 4 // halves * (h + 1))
 
         def regroup(k, c, lo=0, hi=COLS):
             if k < 0 or k >= CELLS:
@@ -271,7 +272,7 @@ def tile_relationnetwork_pa_t_kernel(tc, x, g_W0, g_b0, g_W1, g_b1, out):
                 return
             s = ORDER[k]
             ot = ot_of[k]
-            if k >= CELLS - 2:
+            if k >= CELLS - 4:
                 nc.scalar.activation(out=ot[:, lo:hi, :], in_=ot[:, lo:hi, :], func=ACT.Relu)
             else:
                 nc.vector.tensor_scalar_max(out=ot[:, lo:hi, :], in0=ot[:, lo:hi, :], scalar1=0.0)
@@ -309,33 +310,35 @@ def tile_relationnetwork_pa_t_kernel(tc, x, g_W0, g_b0, g_W1, g_b1, out):
         bias_table()
 
         last = CELLS - 1
+        half = COLS // 2
         for k in range(CELLS):
-            regroup(k - 1, 1)
-            add_bias(k - 3)
-            quantise(k - 1, 1)
-            if k == 0:
-                nc.vector.tensor_copy(out=w1g[:], in_=w1raw[:].rearrange("p (c t) n -> p c n t", t=4))
             layer1(k, 0)
             regroup(k, 0)
+            if k == 0:
+                nc.vector.tensor_copy(out=w1g[:], in_=w1raw[:].rearrange("p (c t) n -> p c n t", t=4))
+            quantise(k - 1, 1)
+            layer2(k - 2)
+            build_pair(k + 2)
+            if k < last:
+                layer1(k, 1)
+                regroup(k, 1)
+            else:
+                layer1(k, 1, 2)
+                regroup(k, 1, 0, half)
             if k == 0:
                 nc.vector.quantize_mx(
                     out=w1w[:].bitcast(FP8X4), scales=w1s[:], in_=w1g[:].rearrange("p c n t -> p (c n t)")
                 )
-            build_pair(k + 2)
-            relu_store(k - 3)
             quantise(k, 0)
-            layer1(k, 1, 2 if k == last else 1)
-            layer2(k - 2)
+            relu_store(k - 3)
+            add_bias(k - 2)
 
-        half = COLS // 2
-        add_bias(last - 2)
         layer2(last - 1)
-        regroup(last, 1, 0, half)
+        regroup(last, 1, half, COLS)
+        quantise(last, 1, 0, half)
         relu_store(last - 2)
         add_bias(last - 1)
-        quantise(last, 1, 0, half)
         relu_store(last - 1)
-        regroup(last, 1, half, COLS)
         layer2(last, 0, 2)
         quantise(last, 1, half, COLS)
         add_bias(last, 0, 2)

@@ -23,6 +23,7 @@ NPB = 4
 REL_MEAN = 0.0
 X_CELLS_ON_VECTOR = 10
 PAIR_SWAP = (1, 0, 3, 2)
+VECTOR_ROW = {4: 3, 6: 3, 10: 0, 12: 0}
 ORDER = [s for s in range(CELLS) if s != 8] + [8]
 
 FLOPS = 2 * B * CELLS * CELLS * (512 * G0 + G0 * G1)
@@ -44,11 +45,11 @@ def tile_relationnetwork_pa_t_kernel(tc, x, g_W0, g_b0, g_W1, g_b1, out):
     with ExitStack() as ctx:
         keep = ctx.enter_context(tc.tile_pool(name="keep", bufs=1))
         planes = ctx.enter_context(tc.tile_pool(name="planes", bufs=6))
-        grouped = ctx.enter_context(tc.tile_pool(name="grouped", bufs=3))
+        grouped = ctx.enter_context(tc.tile_pool(name="grouped", bufs=4))
         packed = ctx.enter_context(tc.tile_pool(name="packed", bufs=6))
         results = ctx.enter_context(tc.tile_pool(name="results", bufs=CELLS))
-        psum1 = ctx.enter_context(tc.psum_pool(name="psum1", bufs=6))
-        psum2 = ctx.enter_context(tc.psum_pool(name="psum2", bufs=2))
+        psum1 = ctx.enter_context(tc.psum_pool(name="psum1", bufs=5))
+        psum2 = ctx.enter_context(tc.psum_pool(name="psum2", bufs=3))
         ctx.enter_context(tc.manual_schedule())
 
         warm = keep.tile([P, 8], F32)
@@ -155,11 +156,64 @@ def tile_relationnetwork_pa_t_kernel(tc, x, g_W0, g_b0, g_W1, g_b1, out):
         words_of = {}
         acc2_of = {}
         ot_of = {}
+        rowacc_of = {}
+
+        def scalar_rows(k):
+            v = VECTOR_ROW.get(ORDER[k])
+            return (1, 4) if v == 0 else (0, 3) if v == 3 else (0, 4)
 
         def new_group(k, c):
             if (k, c) not in group_of:
                 group_of[(k, c)] = grouped.tile([P, COLS, 4], BF16, align_bytes=64, name="hg")
             return group_of[(k, c)]
+
+        def row_matmul(k, c):
+            if ORDER[k] not in VECTOR_ROW:
+                return
+            v = VECTOR_ROW[ORDER[k]]
+            pw, psc = pair_tile(k)
+            acc = psum2.tile([P, 4, P], F32, tag="l2", name="rowacc")
+            rowacc_of[(k, c)] = acc
+            for t in range(4):
+                u = 4 * c + t
+                nc.tensor.matmul_mx(
+                    out=acc[:, t, :],
+                    lhsT=w0w[:, u * P : (u + 1) * P].bitcast(FP8X4),
+                    lhsT_scale=w0s[:, u * P : (u + 1) * P],
+                    rhs=pw[:, v * P : (v + 1) * P].bitcast(FP8X4),
+                    rhs_scale=psc[:, v * P : (v + 1) * P],
+                    start=True,
+                    stop=True,
+                )
+
+        def row_add(k, c):
+            if ORDER[k] not in VECTOR_ROW:
+                return
+            s = ORDER[k]
+            v = VECTOR_ROW[s]
+            acc = rowacc_of[(k, c)]
+            out_v = new_group(k, c)[:, v * P : (v + 1) * P, :]
+            biases = [
+                7 * (dr + 3) + dc + 3
+                for dr, dc, r0, r1, c0, c1 in shift_groups(*divmod(s, 4))
+                if r0 <= v < r1
+            ]
+            n = len(biases)
+            step = biases[n - 1] - biases[0] + (1 if n == 1 else 0)
+            bias = ctab[:].rearrange("p i j u -> p (i j) u")[:, biases[0] : biases[n - 1] + 1 : step, 4 * c : 4 * c + 4]
+            nc.vector.tensor_tensor(
+                out=out_v.rearrange("p (g n) t -> p g n t", g=n),
+                in0=acc[:].rearrange("p t (g n) -> p g n t", g=n),
+                in1=bias.unsqueeze(2).to_broadcast([P, n, P // n, 4]),
+                op=ALU.add,
+            )
+
+        def row_relu(k, c):
+            if ORDER[k] not in VECTOR_ROW:
+                return
+            v = VECTOR_ROW[ORDER[k]]
+            hg = group_of[(k, c)][:, v * P : (v + 1) * P, :].rearrange("p n t -> p (n t)")
+            nc.vector.tensor_scalar_max(out=hg, in0=hg, scalar1=0.0)
 
         def layer1(k, c, halves=1):
             s = ORDER[k]
@@ -168,6 +222,7 @@ def tile_relationnetwork_pa_t_kernel(tc, x, g_W0, g_b0, g_W1, g_b1, out):
             plane = planes.tile([P, 4, COLS], BF16, name="plane")
             plane_of[(k, c)] = plane
             accs = []
+            lo, hi = scalar_rows(k)
 
             def multiply(t):
                 u = 4 * c + t
@@ -207,11 +262,12 @@ def tile_relationnetwork_pa_t_kernel(tc, x, g_W0, g_b0, g_W1, g_b1, out):
             if k > 0:
                 for h in range(halves):
                     for t in PAIR_SWAP:
-                        empty(t, 4 // halves * h, 4 // halves * (h + 1))
+                        empty(t, max(lo, 4 // halves * h), min(hi, 4 // halves * (h + 1)))
 
-        def regroup(k, c, lo=0, hi=COLS):
-            if k < 0 or k >= CELLS:
-                return
+        def regroup(k, c, lo=None, hi=None):
+            if lo is None:
+                r0, r1 = scalar_rows(k)
+                lo, hi = r0 * P, r1 * P
             nc.vector.tensor_copy(
                 out=new_group(k, c)[:, lo:hi, :].rearrange("p (z i) t -> p z t i", i=4),
                 in_=plane_of[(k, c)][:, :, lo:hi].rearrange("p t (z i) -> p z t i", i=4),
@@ -272,7 +328,7 @@ def tile_relationnetwork_pa_t_kernel(tc, x, g_W0, g_b0, g_W1, g_b1, out):
                 return
             s = ORDER[k]
             ot = ot_of[k]
-            if k >= CELLS - 4:
+            if k >= CELLS - 2:
                 nc.scalar.activation(out=ot[:, lo:hi, :], in_=ot[:, lo:hi, :], func=ACT.Relu)
             else:
                 nc.vector.tensor_scalar_max(out=ot[:, lo:hi, :], in0=ot[:, lo:hi, :], scalar1=0.0)
@@ -312,12 +368,16 @@ def tile_relationnetwork_pa_t_kernel(tc, x, g_W0, g_b0, g_W1, g_b1, out):
         last = CELLS - 1
         half = COLS // 2
         for k in range(CELLS):
+            row_matmul(k, 0)
             layer1(k, 0)
             regroup(k, 0)
             if k == 0:
                 nc.vector.tensor_copy(out=w1g[:], in_=w1raw[:].rearrange("p (c t) n -> p c n t", t=4))
+            row_add(k, 0)
             quantise(k - 1, 1)
+            row_relu(k, 0)
             layer2(k - 2)
+            add_bias(k - 2)
             build_pair(k + 2)
             if k < last:
                 layer1(k, 1)
@@ -325,24 +385,25 @@ def tile_relationnetwork_pa_t_kernel(tc, x, g_W0, g_b0, g_W1, g_b1, out):
             else:
                 layer1(k, 1, 2)
                 regroup(k, 1, 0, half)
+            row_matmul(k, 1)
             if k == 0:
                 nc.vector.quantize_mx(
                     out=w1w[:].bitcast(FP8X4), scales=w1s[:], in_=w1g[:].rearrange("p c n t -> p (c n t)")
                 )
+            row_add(k, 1)
             quantise(k, 0)
-            relu_store(k - 3)
-            add_bias(k - 2)
+            row_relu(k, 1)
+            relu_store(k - 2)
 
         layer2(last - 1)
         regroup(last, 1, half, COLS)
         quantise(last, 1, 0, half)
-        relu_store(last - 2)
-        add_bias(last - 1)
-        relu_store(last - 1)
         layer2(last, 0, 2)
         quantise(last, 1, half, COLS)
+        layer2(last, 2, 4)
+        add_bias(last - 1)
+        relu_store(last - 1)
         add_bias(last, 0, 2)
         relu_store(last, 0, 2)
-        layer2(last, 2, 4)
         add_bias(last, 2, 4)
         relu_store(last, 2, 4)

@@ -21,9 +21,7 @@ GT = G0 // P
 COLS = CELLS * B
 NPB = 4
 REL_MEAN = 0.0
-X_CELLS_ON_VECTOR = 10
-PAIR_SWAP = (1, 0, 3, 2)
-VECTOR_ROW = {4: 3, 6: 3, 10: 0, 12: 0}
+VECTOR_ROW = {(s, 0): 3 if s < 8 else 0 for s in range(2, CELLS, 2) if s != 8}
 ORDER = [s for s in range(CELLS) if s != 8] + [8]
 
 FLOPS = 2 * B * CELLS * CELLS * (512 * G0 + G0 * G1)
@@ -53,15 +51,16 @@ def tile_relationnetwork_pa_t_kernel(tc, x, g_W0, g_b0, g_W1, g_b1, out):
         ctx.enter_context(tc.manual_schedule())
 
         warm = keep.tile([P, 8], F32)
-        xraw = keep.tile([P, B, 64], BF16)
+        xraw = keep.tile([P, B // 2, 64], BF16)
+        spread = [keep.tile([P, P], BF16, name="spread%d" % i) for i in range(2)]
         w0raw = keep.tile([P, 4, G0], BF16)
         w1raw = keep.tile([P, GT, G1], BF16)
         brow = keep.tile([P, P], BF16)
         b1bc = keep.tile([P, G1], BF16)
         ident = keep.tile([P, P], BF16)
         delta = keep.tile([P, 7, GT], F32)
-        ow2 = keep.tile([P, 2 * COLS], U32, align_bytes=64)
-        os2 = keep.tile([P, 2 * COLS], U8, align_bytes=64)
+        ow2 = keep.tile([P, COLS], U32, align_bytes=64)
+        os2 = keep.tile([P, COLS], U8, align_bytes=64)
         xg = keep.tile([P, CELLS, B, 4], BF16, align_bytes=64)
         w0g = keep.tile([P, G0, 4], BF16, align_bytes=64)
         w0w = keep.tile([P, G0], U32, align_bytes=64)
@@ -76,40 +75,53 @@ def tile_relationnetwork_pa_t_kernel(tc, x, g_W0, g_b0, g_W1, g_b1, out):
         pws = [keep.tile([P, COLS], U32, align_bytes=64, name="pw%d" % k) for k in range(NPB)]
         pss = [keep.tile([P, COLS], U8, align_bytes=64, name="ps%d" % k) for k in range(NPB)]
 
-        nc.vector.memset(brow[:], 0.0)
+        nc.gpsimd.memset(brow[:], 0.0)
+        nc.vector.memset(warm[:], 0.0)
         nc.vector.memset(os2[:].bitcast(I32), 0)
-        nc.gpsimd.memset(warm[:], 0.0)
         xv = x.rearrange("b (p j) h w -> p b (j h w)", j=4)
-        nc.sync.dma_start(out=xraw[0:64], in_=xv)
-        nc.scalar.dma_start(out=xraw[64:128], in_=xv)
-        nc.scalar.dma_start(out=brow[0:8, :], in_=g_b0.rearrange("(u g) -> u g", g=P))
-        nc.scalar.dma_start(out=brow[8:24, :], in_=g_W0[512:514, :].rearrange("v (u g) -> (v u) g", g=P))
-        nc.scalar.activation(out=warm[:], in_=warm[:], func=ACT.Relu)
-        for h in range(4):
+
+        def load_w0(h):
             nc.sync.dma_start(
                 out=w0raw[:, :, h * 256 : (h + 1) * 256],
                 in_=g_W0[0:512, h * 256 : (h + 1) * 256].rearrange("(p j) g -> p j g", j=4),
             )
+
+        nc.sync.dma_start(out=brow[0:8, :], in_=g_b0.rearrange("(u g) -> u g", g=P))
+        nc.sync.dma_start(out=brow[8:24, :], in_=g_W0[512:514, :].rearrange("v (u g) -> (v u) g", g=P))
+        nc.sync.dma_start(out=xraw[0:64], in_=xv[:, 0 : B // 2])
+        nc.scalar.dma_start(out=xraw[64:128], in_=xv[:, B // 2 : B])
+        nc.scalar.activation(out=warm[:], in_=warm[:], func=ACT.Relu)
+        load_w0(0)
+        load_w0(1)
+        load_w0(2)
+        load_w0(3)
         nc.sync.dma_start(out=w1raw[:], in_=g_W1.rearrange("(u p) n -> p u n", p=P))
         nc.sync.dma_start(out=b1bc[:], in_=g_b1.partition_broadcast(P))
 
         make_identity(nc, ident[:])
+        for i in range(2):
+            for m in range(2):
+                nc.gpsimd.tensor_copy(out=spread[i][:, 64 * m : 64 * m + 64], in_=ident[:, 64 * i : 64 * i + 64])
         for i in range(7):
             nc.gpsimd.memset(delta[:, i, :], float(i - 3) - REL_MEAN)
 
         bt_ps = psum2.tile([P, P], BF16, tag="l2")
         nc.tensor.transpose(bt_ps[:], brow[:], ident[:])
 
-        def bias_table():
+        def bias_rows():
             nc.vector.tensor_tensor(
                 out=row_part[:], in0=delta[:], in1=bt[:, 8:16].unsqueeze(1).to_broadcast([P, 7, GT]), op=ALU.mult
             )
             nc.vector.tensor_tensor(
                 out=col_part[:], in0=delta[:], in1=bt[:, 16:24].unsqueeze(1).to_broadcast([P, 7, GT]), op=ALU.mult
             )
+
+        def bias_base():
             nc.vector.tensor_tensor(
                 out=row_part[:], in0=row_part[:], in1=bt[:, 0:8].unsqueeze(1).to_broadcast([P, 7, GT]), op=ALU.add
             )
+
+        def bias_table():
             nc.vector.tensor_tensor(
                 out=ctab[:],
                 in0=row_part[:].unsqueeze(2).to_broadcast([P, 7, 7, GT]),
@@ -117,27 +129,22 @@ def tile_relationnetwork_pa_t_kernel(tc, x, g_W0, g_b0, g_W1, g_b1, out):
                 op=ALU.add,
             )
 
-        def w0_regroup(engine_copy, h):
-            cols = slice(h * 256, (h + 1) * 256)
+        def w0_regroup(engine_copy, lo, hi):
             engine_copy(
-                out=w0g[:, cols, :].rearrange("p (c i) j -> p c j i", i=4),
-                in_=w0raw[:, :, cols].rearrange("p j (c i) -> p c j i", i=4),
+                out=w0g[:, lo * P : hi * P, :].rearrange("p (c i) j -> p c j i", i=4),
+                in_=w0raw[:, :, lo * P : hi * P].rearrange("p j (c i) -> p c j i", i=4),
             )
 
-        def w0_quantise(h):
-            cols = slice(h * 256, (h + 1) * 256)
+        def w0_quantise(lo, hi):
             nc.vector.quantize_mx(
-                out=w0w[:, cols].bitcast(FP8X4),
-                scales=w0s[:, cols],
-                in_=w0g[:, cols, :].rearrange("p g j -> p (g j)"),
+                out=w0w[:, lo * P : hi * P].bitcast(FP8X4),
+                scales=w0s[:, lo * P : hi * P],
+                in_=w0g[:, lo * P : hi * P, :].rearrange("p g j -> p (g j)"),
             )
-
-        def move(dst, src):
-            nc.vector.tensor_copy(out=dst.bitcast(I32), in_=src.bitcast(I32))
 
         def pair_tile(k):
             if k == 0:
-                return ow2[:, 0:COLS], os2[:, 0:COLS]
+                return ow2[:], os2[:]
             return pws[k % NPB][:], pss[k % NPB][:]
 
         def build_pair(k):
@@ -145,11 +152,16 @@ def tile_relationnetwork_pa_t_kernel(tc, x, g_W0, g_b0, g_W1, g_b1, out):
                 return
             s = ORDER[k]
             pw, psc = pair_tile(k)
-            if k <= NPB:
-                nc.sync.dma_start(out=pw[0:64, :].bitcast(I32), in_=ow2[0:64, 0:COLS].bitcast(I32))
-                nc.sync.dma_start(out=psc[0:64, :].bitcast(I32), in_=os2[0:64, 0:COLS].bitcast(I32))
-            nc.sync.dma_start(out=pw[64:128, :].bitcast(I32), in_=ow2[64:128, s * B : s * B + COLS].bitcast(I32))
-            nc.sync.dma_start(out=psc[64:128, :].bitcast(I32), in_=os2[64:128, s * B : s * B + COLS].bitcast(I32))
+            def move(dst, src, rows, d0, d1, s0):
+                nc.sync.dma_start(
+                    out=dst[rows, d0:d1].bitcast(I32), in_=src[rows, s0 : s0 + d1 - d0].bitcast(I32)
+                )
+
+            for dst, src in ((pw, ow2), (psc, os2)):
+                if k <= NPB:
+                    move(dst, src, slice(0, 64), 0, COLS, 0)
+                move(dst, src, slice(64, 128), 0, COLS - s * B, s * B)
+                move(dst, src, slice(64, 128), COLS - s * B, COLS, 0)
 
         plane_of = {}
         group_of = {}
@@ -158,8 +170,8 @@ def tile_relationnetwork_pa_t_kernel(tc, x, g_W0, g_b0, g_W1, g_b1, out):
         ot_of = {}
         rowacc_of = {}
 
-        def scalar_rows(k):
-            v = VECTOR_ROW.get(ORDER[k])
+        def scalar_rows(k, c):
+            v = VECTOR_ROW.get((ORDER[k], c))
             return (1, 4) if v == 0 else (0, 3) if v == 3 else (0, 4)
 
         def new_group(k, c):
@@ -168,9 +180,9 @@ def tile_relationnetwork_pa_t_kernel(tc, x, g_W0, g_b0, g_W1, g_b1, out):
             return group_of[(k, c)]
 
         def row_matmul(k, c):
-            if ORDER[k] not in VECTOR_ROW:
+            if (ORDER[k], c) not in VECTOR_ROW:
                 return
-            v = VECTOR_ROW[ORDER[k]]
+            v = VECTOR_ROW[ORDER[k], c]
             pw, psc = pair_tile(k)
             acc = psum2.tile([P, 4, P], F32, tag="l2", name="rowacc")
             rowacc_of[(k, c)] = acc
@@ -187,31 +199,25 @@ def tile_relationnetwork_pa_t_kernel(tc, x, g_W0, g_b0, g_W1, g_b1, out):
                 )
 
         def row_add(k, c):
-            if ORDER[k] not in VECTOR_ROW:
+            if (ORDER[k], c) not in VECTOR_ROW:
                 return
             s = ORDER[k]
-            v = VECTOR_ROW[s]
+            v = VECTOR_ROW[s, c]
             acc = rowacc_of[(k, c)]
             out_v = new_group(k, c)[:, v * P : (v + 1) * P, :]
-            biases = [
-                7 * (dr + 3) + dc + 3
-                for dr, dc, r0, r1, c0, c1 in shift_groups(*divmod(s, 4))
-                if r0 <= v < r1
-            ]
-            n = len(biases)
-            step = biases[n - 1] - biases[0] + (1 if n == 1 else 0)
-            bias = ctab[:].rearrange("p i j u -> p (i j) u")[:, biases[0] : biases[n - 1] + 1 : step, 4 * c : 4 * c + 4]
-            nc.vector.tensor_tensor(
-                out=out_v.rearrange("p (g n) t -> p g n t", g=n),
-                in0=acc[:].rearrange("p t (g n) -> p g n t", g=n),
-                in1=bias.unsqueeze(2).to_broadcast([P, n, P // n, 4]),
-                op=ALU.add,
-            )
+            parts = [g for g in shift_groups(*divmod(s, 4)) if g[2] <= v < g[3]]
+            for dr, dc, r0, r1, c0, c1 in parts:
+                nc.vector.tensor_tensor(
+                    out=out_v[:, B * c0 : B * c1, :],
+                    in0=acc[:].rearrange("p t n -> p n t")[:, B * c0 : B * c1, :],
+                    in1=ctab[:, dr + 3, dc + 3, 4 * c : 4 * c + 4].unsqueeze(1).to_broadcast([P, B * (c1 - c0), 4]),
+                    op=ALU.add,
+                )
 
         def row_relu(k, c):
-            if ORDER[k] not in VECTOR_ROW:
+            if (ORDER[k], c) not in VECTOR_ROW:
                 return
-            v = VECTOR_ROW[ORDER[k]]
+            v = VECTOR_ROW[ORDER[k], c]
             hg = group_of[(k, c)][:, v * P : (v + 1) * P, :].rearrange("p n t -> p (n t)")
             nc.vector.tensor_scalar_max(out=hg, in0=hg, scalar1=0.0)
 
@@ -222,7 +228,7 @@ def tile_relationnetwork_pa_t_kernel(tc, x, g_W0, g_b0, g_W1, g_b1, out):
             plane = planes.tile([P, 4, COLS], BF16, name="plane")
             plane_of[(k, c)] = plane
             accs = []
-            lo, hi = scalar_rows(k)
+            lo, hi = scalar_rows(k, c)
 
             def multiply(t):
                 u = 4 * c + t
@@ -257,18 +263,18 @@ def tile_relationnetwork_pa_t_kernel(tc, x, g_W0, g_b0, g_W1, g_b1, out):
 
             for t in range(4):
                 multiply(t)
-                if k == 0:
-                    empty(t, 0, 4)
-            if k > 0:
-                for h in range(halves):
-                    for t in PAIR_SWAP:
-                        empty(t, max(lo, 4 // halves * h), min(hi, 4 // halves * (h + 1)))
+                if halves == 1:
+                    empty(t, lo, hi)
+            if halves == 2:
+                for h in range(2):
+                    for t in range(4):
+                        empty(t, 2 * h, 2 * h + 2)
 
-        def regroup(k, c, lo=None, hi=None):
+        def regroup(k, c, lo=None, hi=None, copy=nc.vector.tensor_copy):
             if lo is None:
-                r0, r1 = scalar_rows(k)
+                r0, r1 = scalar_rows(k, c)
                 lo, hi = r0 * P, r1 * P
-            nc.vector.tensor_copy(
+            copy(
                 out=new_group(k, c)[:, lo:hi, :].rearrange("p (z i) t -> p z t i", i=4),
                 in_=plane_of[(k, c)][:, :, lo:hi].rearrange("p t (z i) -> p z t i", i=4),
             )
@@ -344,26 +350,36 @@ def tile_relationnetwork_pa_t_kernel(tc, x, g_W0, g_b0, g_W1, g_b1, out):
                         in_=ot[B * c : B * (c + 1), r0:r1, :],
                     )
 
-        xr = xraw[:].rearrange("p b (j n) -> p n b j", j=4)
-        nv = X_CELLS_ON_VECTOR
-        nc.vector.tensor_copy(out=xg[:, 0:nv], in_=xr[:, 0:nv])
-        nc.scalar.copy(out=xg[:, nv:CELLS], in_=xr[:, nv:CELLS])
-        w0_regroup(nc.vector.tensor_copy, 0)
-        w0_regroup(nc.scalar.copy, 1)
-        nc.vector.quantize_mx(
-            out=ow2[:, 0:COLS].bitcast(FP8X4), scales=os2[:, 0:COLS], in_=xg[:].rearrange("p n b j -> p (n b j)")
-        )
-        w0_quantise(0)
         nc.vector.tensor_copy(out=bt[:], in_=bt_ps[:, 0:24])
-        w0_quantise(1)
-        move(ow2[64:128, COLS : 2 * COLS], ow2[64:128, 0:COLS])
-        move(os2[64:128, COLS : 2 * COLS], os2[64:128, 0:COLS])
-        w0_regroup(nc.vector.tensor_copy, 2)
-        w0_regroup(nc.vector.tensor_copy, 3)
-        w0_quantise(2)
-        w0_quantise(3)
-        build_pair(1)
+        bias_rows()
+        bias_base()
         bias_table()
+        for i in range(4):
+            xacc = psum1.tile([P, COLS], F32, name="acc")
+            nc.tensor.matmul(
+                out=xacc[:],
+                lhsT=spread[i // 2][:],
+                rhs=xraw[:, 8 * (i % 2) : 8 * (i % 2) + 8, :].rearrange("p b z -> p (b z)"),
+                start=True,
+                stop=True,
+            )
+            copy = nc.scalar.copy if i % 2 else nc.vector.tensor_copy
+            copy(
+                out=xg[:, :, 8 * i : 8 * i + 8, :], in_=xacc[:].rearrange("p (b j n) -> p n b j", b=8, j=4)
+            )
+        w0_regroup(nc.vector.tensor_copy, 0, 1)
+        w0_regroup(nc.vector.tensor_copy, 1, 2)
+        w0_quantise(0, 1)
+        nc.vector.quantize_mx(out=ow2[:].bitcast(FP8X4), scales=os2[:], in_=xg[:].rearrange("p n b j -> p (n b j)"))
+        w0_regroup(nc.scalar.copy, 2, 4)
+        w0_quantise(1, 2)
+        w0_regroup(nc.vector.tensor_copy, 4, 6)
+        w0_quantise(2, 4)
+        w0_regroup(nc.vector.tensor_copy, 6, 8)
+        w0_quantise(4, 6)
+        w0_quantise(6, 8)
+        build_pair(1)
+        build_pair(2)
 
         last = CELLS - 1
         half = COLS // 2
@@ -378,7 +394,7 @@ def tile_relationnetwork_pa_t_kernel(tc, x, g_W0, g_b0, g_W1, g_b1, out):
             row_relu(k, 0)
             layer2(k - 2)
             add_bias(k - 2)
-            build_pair(k + 2)
+            build_pair(k + 3)
             if k < last:
                 layer1(k, 1)
                 regroup(k, 1)
@@ -391,18 +407,21 @@ def tile_relationnetwork_pa_t_kernel(tc, x, g_W0, g_b0, g_W1, g_b1, out):
                     out=w1w[:].bitcast(FP8X4), scales=w1s[:], in_=w1g[:].rearrange("p c n t -> p (c n t)")
                 )
             row_add(k, 1)
+            if k == last:
+                relu_store(k - 2)
             quantise(k, 0)
             row_relu(k, 1)
-            relu_store(k - 2)
+            if k < last:
+                relu_store(k - 2)
 
         layer2(last - 1)
-        regroup(last, 1, half, COLS)
+        regroup(last, 1, half, COLS, nc.scalar.copy)
+        add_bias(last - 1)
+        relu_store(last - 1)
         quantise(last, 1, 0, half)
         layer2(last, 0, 2)
         quantise(last, 1, half, COLS)
         layer2(last, 2, 4)
-        add_bias(last - 1)
-        relu_store(last - 1)
         add_bias(last, 0, 2)
         relu_store(last, 0, 2)
         add_bias(last, 2, 4)

@@ -21,8 +21,8 @@ GT = G0 // P
 COLS = CELLS * B
 NPB = 4
 REL_MEAN = 0.0
-VECTOR_ROW = {(s, 0): 3 if s < 8 else 0 for s in range(2, CELLS, 2) if s != 8}
 ORDER = [s for s in range(CELLS) if s != 8] + [8]
+VECTOR_ROW = {(s, 0): 3 if s < 8 else 0 for s in ORDER[1:14:2]}
 
 FLOPS = 2 * B * CELLS * CELLS * (512 * G0 + G0 * G1)
 
@@ -88,10 +88,10 @@ def tile_relationnetwork_pa_t_kernel(tc, x, g_W0, g_b0, g_W1, g_b1, out):
 
         nc.sync.dma_start(out=brow[0:8, :], in_=g_b0.rearrange("(u g) -> u g", g=P))
         nc.sync.dma_start(out=brow[8:24, :], in_=g_W0[512:514, :].rearrange("v (u g) -> (v u) g", g=P))
+        load_w0(0)
         nc.sync.dma_start(out=xraw[0:64], in_=xv[:, 0 : B // 2])
         nc.scalar.dma_start(out=xraw[64:128], in_=xv[:, B // 2 : B])
         nc.scalar.activation(out=warm[:], in_=warm[:], func=ACT.Relu)
-        load_w0(0)
         load_w0(1)
         load_w0(2)
         load_w0(3)
@@ -230,16 +230,16 @@ def tile_relationnetwork_pa_t_kernel(tc, x, g_W0, g_b0, g_W1, g_b1, out):
             accs = []
             lo, hi = scalar_rows(k, c)
 
-            def multiply(t):
+            def multiply(t, z0=0, z1=COLS):
                 u = 4 * c + t
-                acc = psum1.tile([P, COLS], F32, name="acc")
-                accs.append(acc)
+                if z0 == 0:
+                    accs.append(psum1.tile([P, COLS], F32, name="acc"))
                 nc.tensor.matmul_mx(
-                    out=acc[:],
+                    out=accs[t][:, z0:z1],
                     lhsT=w0w[:, u * P : (u + 1) * P].bitcast(FP8X4),
                     lhsT_scale=w0s[:, u * P : (u + 1) * P],
-                    rhs=pw.bitcast(FP8X4),
-                    rhs_scale=psc,
+                    rhs=pw[:, z0:z1].bitcast(FP8X4),
+                    rhs_scale=psc[:, z0:z1],
                     start=True,
                     stop=True,
                 )
@@ -261,6 +261,12 @@ def tile_relationnetwork_pa_t_kernel(tc, x, g_W0, g_b0, g_W1, g_b1, out):
                         scale=1.0,
                     )
 
+            if k == 0 and c == 0:
+                for h in range(2):
+                    for t in range(4):
+                        multiply(t, 256 * h, 256 * h + 256)
+                        empty(t, 2 * h, 2 * h + 2)
+                return
             for t in range(4):
                 multiply(t)
                 if halves == 1:
@@ -350,10 +356,14 @@ def tile_relationnetwork_pa_t_kernel(tc, x, g_W0, g_b0, g_W1, g_b1, out):
                         in_=ot[B * c : B * (c + 1), r0:r1, :],
                     )
 
+        w0_regroup(nc.vector.tensor_copy, 0, 1)
         nc.vector.tensor_copy(out=bt[:], in_=bt_ps[:, 0:24])
+        w0_regroup(nc.vector.tensor_copy, 1, 2)
         bias_rows()
+        w0_quantise(0, 2)
         bias_base()
-        bias_table()
+        w0_regroup(nc.vector.tensor_copy, 2, 3)
+        xaccs = []
         for i in range(4):
             xacc = psum1.tile([P, COLS], F32, name="acc")
             nc.tensor.matmul(
@@ -363,19 +373,37 @@ def tile_relationnetwork_pa_t_kernel(tc, x, g_W0, g_b0, g_W1, g_b1, out):
                 start=True,
                 stop=True,
             )
+            xaccs.append(xacc)
+
+        def x_copy(i, h):
             copy = nc.scalar.copy if i % 2 else nc.vector.tensor_copy
             copy(
-                out=xg[:, :, 8 * i : 8 * i + 8, :], in_=xacc[:].rearrange("p (b j n) -> p n b j", b=8, j=4)
+                out=xg[:, 8 * h : 8 * h + 8, 8 * i : 8 * i + 8, :],
+                in_=xaccs[i][:].rearrange("p (b j n) -> p n b j", b=8, j=4)[:, 8 * h : 8 * h + 8],
             )
-        w0_regroup(nc.vector.tensor_copy, 0, 1)
-        w0_regroup(nc.vector.tensor_copy, 1, 2)
-        w0_quantise(0, 1)
-        nc.vector.quantize_mx(out=ow2[:].bitcast(FP8X4), scales=os2[:], in_=xg[:].rearrange("p n b j -> p (n b j)"))
-        w0_regroup(nc.scalar.copy, 2, 4)
-        w0_quantise(1, 2)
-        w0_regroup(nc.vector.tensor_copy, 4, 6)
+
+        def x_quantise(h):
+            nc.vector.quantize_mx(
+                out=ow2[:, 256 * h : 256 * h + 256].bitcast(FP8X4),
+                scales=os2[:, 256 * h : 256 * h + 256],
+                in_=xg[:, 8 * h : 8 * h + 8].rearrange("p n b j -> p (n b j)"),
+            )
+
+        x_copy(0, 0)
+        x_copy(1, 0)
+        x_copy(2, 0)
+        x_copy(3, 0)
+        w0_regroup(nc.vector.tensor_copy, 3, 4)
+        x_copy(0, 1)
+        x_copy(1, 1)
+        x_quantise(0)
+        x_copy(2, 1)
+        x_copy(3, 1)
+        w0_regroup(nc.scalar.copy, 4, 6)
         w0_quantise(2, 4)
+        x_quantise(1)
         w0_regroup(nc.vector.tensor_copy, 6, 8)
+        bias_table()
         w0_quantise(4, 6)
         w0_quantise(6, 8)
         build_pair(1)
@@ -386,7 +414,8 @@ def tile_relationnetwork_pa_t_kernel(tc, x, g_W0, g_b0, g_W1, g_b1, out):
         for k in range(CELLS):
             row_matmul(k, 0)
             layer1(k, 0)
-            regroup(k, 0)
+            if k < last:
+                regroup(k, 0)
             if k == 0:
                 nc.vector.tensor_copy(out=w1g[:], in_=w1raw[:].rearrange("p (c t) n -> p c n t", t=4))
             row_add(k, 0)
@@ -398,26 +427,25 @@ def tile_relationnetwork_pa_t_kernel(tc, x, g_W0, g_b0, g_W1, g_b1, out):
             if k < last:
                 layer1(k, 1)
                 regroup(k, 1)
-            else:
-                layer1(k, 1, 2)
-                regroup(k, 1, 0, half)
-            row_matmul(k, 1)
-            if k == 0:
-                nc.vector.quantize_mx(
-                    out=w1w[:].bitcast(FP8X4), scales=w1s[:], in_=w1g[:].rearrange("p c n t -> p (c n t)")
-                )
-            row_add(k, 1)
-            if k == last:
-                relu_store(k - 2)
-            quantise(k, 0)
-            row_relu(k, 1)
-            if k < last:
+                if k == 0:
+                    nc.vector.quantize_mx(
+                        out=w1w[:].bitcast(FP8X4), scales=w1s[:], in_=w1g[:].rearrange("p c n t -> p (c n t)")
+                    )
+                row_matmul(k, 1)
+                row_add(k, 1)
+                quantise(k, 0)
+                row_relu(k, 1)
                 relu_store(k - 2)
 
+        layer1(last, 1, 2)
         layer2(last - 1)
+        regroup(last, 0)
+        relu_store(last - 2)
+        regroup(last, 1, 0, half)
         regroup(last, 1, half, COLS, nc.scalar.copy)
         add_bias(last - 1)
         relu_store(last - 1)
+        quantise(last, 0)
         quantise(last, 1, 0, half)
         layer2(last, 0, 2)
         quantise(last, 1, half, COLS)

@@ -281,8 +281,8 @@ def tile_relationnetwork_pa_t_kernel(tc, x, g_W0, g_b0, g_W1, g_b1, out):
                 r0, r1 = scalar_rows(k, c)
                 lo, hi = r0 * P, r1 * P
             copy(
-                out=new_group(k, c)[:, lo:hi, :].rearrange("p (z i) t -> p z t i", i=4),
-                in_=plane_of[(k, c)][:, :, lo:hi].rearrange("p t (z i) -> p z t i", i=4),
+                out=new_group(k, c)[:, lo:hi, :].rearrange("p (z i) t -> p z t i", i=8),
+                in_=plane_of[(k, c)][:, :, lo:hi].rearrange("p t (z i) -> p z t i", i=8),
             )
 
         def quantise(k, c, lo=0, hi=COLS):

from contextlib import ExitStack

import concourse.mybir as mybir
from concourse.masks import make_identity

F32 = mybir.dt.float32
BF16 = mybir.dt.bfloat16
U32 = mybir.dt.uint32
U8 = mybir.dt.uint8
I32 = mybir.dt.int32
FP8X4 = mybir.dt.float8_e4m3fn_x4
ACT = mybir.ActivationFunctionType
ALU = mybir.AluOpType

P = 128
B = 32
CELLS = 16
G0 = 1024
G1 = 128
GT = G0 // P
COLS = CELLS * B
NPB = 4
REL_MEAN = 0.0
ORDER = [s for s in range(CELLS) if s != 8] + [8]
VECTOR_ROW = {(s, 0): 3 if s < 8 else 0 for s in ORDER[1:14:2]}

FLOPS = 2 * B * CELLS * CELLS * (512 * G0 + G0 * G1)


def shift_groups(a, d):
    found = [(a, d, 0, 4 - a, 0, 4 - d)]
    if d > 0 and a < 3:
        found.append((a + 1, d - 4, 0, 3 - a, 4 - d, 4))
    if a > 0:
        found.append((a - 4, d, 4 - a, 4, 0, 4 - d))
    if d > 0:
        found.append((a - 3, d - 4, 3 - a, 4, 4 - d, 4))
    return found


def tile_relationnetwork_pa_t_kernel(tc, x, g_W0, g_b0, g_W1, g_b1, out):
    nc = tc.nc
    with ExitStack() as ctx:
        keep = ctx.enter_context(tc.tile_pool(name="keep", bufs=1))
        planes = ctx.enter_context(tc.tile_pool(name="planes", bufs=6))
        grouped = ctx.enter_context(tc.tile_pool(name="grouped", bufs=4))
        packed = ctx.enter_context(tc.tile_pool(name="packed", bufs=6))
        results = ctx.enter_context(tc.tile_pool(name="results", bufs=CELLS))
        psum1 = ctx.enter_context(tc.psum_pool(name="psum1", bufs=5))
        psum2 = ctx.enter_context(tc.psum_pool(name="psum2", bufs=3))
        ctx.enter_context(tc.manual_schedule())

        warm = keep.tile([P, 8], F32)
        xraw = keep.tile([P, B // 2, 64], BF16)
        spread = [keep.tile([P, P], BF16, name="spread%d" % i) for i in range(2)]
        w0raw = keep.tile([P, 4, G0], BF16)
        w1raw = keep.tile([P, GT, G1], BF16)
        brow = keep.tile([P, P], BF16)
        b1bc = keep.tile([P, G1], BF16)
        ident = keep.tile([P, P], BF16)
        delta = keep.tile([P, 7, GT], F32)
        ow2 = keep.tile([P, COLS], U32, align_bytes=64)
        os2 = keep.tile([P, COLS], U8, align_bytes=64)
        xg = keep.tile([P, CELLS, B, 4], BF16, align_bytes=64)
        w0g = keep.tile([P, G0, 4], BF16, align_bytes=64)
        w0w = keep.tile([P, G0], U32, align_bytes=64)
        w0s = keep.tile([P, G0], U8, align_bytes=64)
        bt = keep.tile([P, 24], F32)
        row_part = keep.tile([P, 7, GT], F32)
        col_part = keep.tile([P, 7, GT], F32)
        ctab = keep.tile([P, 7, 7, GT], F32)
        w1g = keep.tile([P, 2, G1, 4], BF16, align_bytes=64)
        w1w = keep.tile([P, 2 * G1], U32, align_bytes=64)
        w1s = keep.tile([P, 2 * G1], U8, align_bytes=64)
        pws = [keep.tile([P, COLS], U32, align_bytes=64, name="pw%d" % k) for k in range(NPB)]
        pss = [keep.tile([P, COLS], U8, align_bytes=64, name="ps%d" % k) for k in range(NPB)]

        nc.gpsimd.memset(brow[:], 0.0)
        nc.vector.memset(warm[:], 0.0)
        nc.vector.memset(os2[:].bitcast(I32), 0)
        xv = x.rearrange("b (p j) h w -> p b (j h w)", j=4)

        def load_w0(h):
            nc.sync.dma_start(
                out=w0raw[:, :, h * 256 : (h + 1) * 256],
                in_=g_W0[0:512, h * 256 : (h + 1) * 256].rearrange("(p j) g -> p j g", j=4),
            )

        nc.sync.dma_start(out=brow[0:8, :], in_=g_b0.rearrange("(u g) -> u g", g=P))
        nc.sync.dma_start(out=brow[8:24, :], in_=g_W0[512:514, :].rearrange("v (u g) -> (v u) g", g=P))
        load_w0(0)
        nc.sync.dma_start(out=xraw[0:64], in_=xv[:, 0 : B // 2])
        nc.scalar.dma_start(out=xraw[64:128], in_=xv[:, B // 2 : B])
        nc.scalar.activation(out=warm[:], in_=warm[:], func=ACT.Relu)
        load_w0(1)
        load_w0(2)
        load_w0(3)
        nc.sync.dma_start(out=w1raw[:], in_=g_W1.rearrange("(u p) n -> p u n", p=P))
        nc.sync.dma_start(out=b1bc[:], in_=g_b1.partition_broadcast(P))

        make_identity(nc, ident[:])
        for i in range(2):
            for m in range(2):
                nc.gpsimd.tensor_copy(out=spread[i][:, 64 * m : 64 * m + 64], in_=ident[:, 64 * i : 64 * i + 64])
        for i in range(7):
            nc.gpsimd.memset(delta[:, i, :], float(i - 3) - REL_MEAN)

        bt_ps = psum2.tile([P, P], BF16, tag="l2")
        nc.tensor.transpose(bt_ps[:], brow[:], ident[:])

        def bias_rows():
            nc.vector.tensor_tensor(
                out=row_part[:], in0=delta[:], in1=bt[:, 8:16].unsqueeze(1).to_broadcast([P, 7, GT]), op=ALU.mult
            )
            nc.vector.tensor_tensor(
                out=col_part[:], in0=delta[:], in1=bt[:, 16:24].unsqueeze(1).to_broadcast([P, 7, GT]), op=ALU.mult
            )

        def bias_base():
            nc.vector.tensor_tensor(
                out=row_part[:], in0=row_part[:], in1=bt[:, 0:8].unsqueeze(1).to_broadcast([P, 7, GT]), op=ALU.add
            )

        def bias_table():
            nc.vector.tensor_tensor(
                out=ctab[:],
                in0=row_part[:].unsqueeze(2).to_broadcast([P, 7, 7, GT]),
                in1=col_part[:].unsqueeze(1).to_broadcast([P, 7, 7, GT]),
                op=ALU.add,
            )

        def w0_regroup(engine_copy, lo, hi):
            engine_copy(
                out=w0g[:, lo * P : hi * P, :].rearrange("p (c i) j -> p c j i", i=4),
                in_=w0raw[:, :, lo * P : hi * P].rearrange("p j (c i) -> p c j i", i=4),
            )

        def w0_quantise(lo, hi):
            nc.vector.quantize_mx(
                out=w0w[:, lo * P : hi * P].bitcast(FP8X4),
                scales=w0s[:, lo * P : hi * P],
                in_=w0g[:, lo * P : hi * P, :].rearrange("p g j -> p (g j)"),
            )

        def pair_tile(k):
            if k == 0:
                return ow2[:], os2[:]
            return pws[k % NPB][:], pss[k % NPB][:]

        def build_pair(k):
            if k >= CELLS:
                return
            s = ORDER[k]
            pw, psc = pair_tile(k)
            def move(dst, src, rows, d0, d1, s0):
                nc.sync.dma_start(
                    out=dst[rows, d0:d1].bitcast(I32), in_=src[rows, s0 : s0 + d1 - d0].bitcast(I32)
                )

            for dst, src in ((pw, ow2), (psc, os2)):
                if k <= NPB:
                    move(dst, src, slice(0, 64), 0, COLS, 0)
                move(dst, src, slice(64, 128), 0, COLS - s * B, s * B)
                move(dst, src, slice(64, 128), COLS - s * B, COLS, 0)

        plane_of = {}
        group_of = {}
        words_of = {}
        acc2_of = {}
        ot_of = {}
        rowacc_of = {}

        def scalar_rows(k, c):
            v = VECTOR_ROW.get((ORDER[k], c))
            return (1, 4) if v == 0 else (0, 3) if v == 3 else (0, 4)

        def new_group(k, c):
            if (k, c) not in group_of:
                group_of[(k, c)] = grouped.tile([P, COLS, 4], BF16, align_bytes=64, name="hg")
            return group_of[(k, c)]

        def row_matmul(k, c):
            if (ORDER[k], c) not in VECTOR_ROW:
                return
            v = VECTOR_ROW[ORDER[k], c]
            pw, psc = pair_tile(k)
            acc = psum2.tile([P, 4, P], F32, tag="l2", name="rowacc")
            rowacc_of[(k, c)] = acc
            for t in range(4):
                u = 4 * c + t
                nc.tensor.matmul_mx(
                    out=acc[:, t, :],
                    lhsT=w0w[:, u * P : (u + 1) * P].bitcast(FP8X4),
                    lhsT_scale=w0s[:, u * P : (u + 1) * P],
                    rhs=pw[:, v * P : (v + 1) * P].bitcast(FP8X4),
                    rhs_scale=psc[:, v * P : (v + 1) * P],
                    start=True,
                    stop=True,
                )

        def row_add(k, c):
            if (ORDER[k], c) not in VECTOR_ROW:
                return
            s = ORDER[k]
            v = VECTOR_ROW[s, c]
            acc = rowacc_of[(k, c)]
            out_v = new_group(k, c)[:, v * P : (v + 1) * P, :]
            parts = [g for g in shift_groups(*divmod(s, 4)) if g[2] <= v < g[3]]
            for dr, dc, r0, r1, c0, c1 in parts:
                nc.vector.tensor_tensor(
                    out=out_v[:, B * c0 : B * c1, :],
                    in0=acc[:].rearrange("p t n -> p n t")[:, B * c0 : B * c1, :],
                    in1=ctab[:, dr + 3, dc + 3, 4 * c : 4 * c + 4].unsqueeze(1).to_broadcast([P, B * (c1 - c0), 4]),
                    op=ALU.add,
                )

        def row_relu(k, c):
            if (ORDER[k], c) not in VECTOR_ROW:
                return
            v = VECTOR_ROW[ORDER[k], c]
            hg = group_of[(k, c)][:, v * P : (v + 1) * P, :].rearrange("p n t -> p (n t)")
            nc.vector.tensor_scalar_max(out=hg, in0=hg, scalar1=0.0)

        def layer1(k, c, halves=1):
            s = ORDER[k]
            a, d = divmod(s, 4)
            pw, psc = pair_tile(k)
            plane = planes.tile([P, 4, COLS], BF16, name="plane")
            plane_of[(k, c)] = plane
            accs = []
            lo, hi = scalar_rows(k, c)

            def multiply(t, z0=0, z1=COLS):
                u = 4 * c + t
                if z0 == 0:
                    accs.append(psum1.tile([P, COLS], F32, name="acc"))
                nc.tensor.matmul_mx(
                    out=accs[t][:, z0:z1],
                    lhsT=w0w[:, u * P : (u + 1) * P].bitcast(FP8X4),
                    lhsT_scale=w0s[:, u * P : (u + 1) * P],
                    rhs=pw[:, z0:z1].bitcast(FP8X4),
                    rhs_scale=psc[:, z0:z1],
                    start=True,
                    stop=True,
                )

            def empty(t, lo, hi):
                u = 4 * c + t
                acc_v = accs[t][:].rearrange("p (r z) -> p r z", r=4)
                pl_v = plane[:, t, :].rearrange("p (r z) -> p r z", r=4)
                for dr, dc, r0, r1, c0, c1 in shift_groups(a, d):
                    r0, r1 = max(r0, lo), min(r1, hi)
                    if r1 <= r0:
                        continue
                    bias = bt[:, u : u + 1] if s == 0 else ctab[:, dr + 3, dc + 3, u : u + 1]
                    nc.scalar.activation(
                        out=pl_v[:, r0:r1, B * c0 : B * c1],
                        in_=acc_v[:, r0:r1, B * c0 : B * c1],
                        func=ACT.Relu,
                        bias=bias,
                        scale=1.0,
                    )

            if k == 0 and c == 0:
                for h in range(2):
                    for t in range(4):
                        multiply(t, 256 * h, 256 * h + 256)
                        empty(t, 2 * h, 2 * h + 2)
                return
            for t in range(4):
                multiply(t)
                if halves == 1:
                    empty(t, lo, hi)
            if halves == 2:
                for h in range(2):
                    for t in range(4):
                        empty(t, 2 * h, 2 * h + 2)

        def regroup(k, c, lo=None, hi=None, copy=nc.vector.tensor_copy):
            if lo is None:
                r0, r1 = scalar_rows(k, c)
                lo, hi = r0 * P, r1 * P
            copy(
                out=new_group(k, c)[:, lo:hi, :].rearrange("p (z i) t -> p z t i", i=8),
                in_=plane_of[(k, c)][:, :, lo:hi].rearrange("p t (z i) -> p z t i", i=8),
            )

        def quantise(k, c, lo=0, hi=COLS):
            if k < 0 or k >= CELLS:
                return
            if lo == 0:
                words_of[(k, c)] = (
                    packed.tile([P, COLS], U32, align_bytes=64, name="hw"),
                    packed.tile([P, COLS], U8, align_bytes=64, name="hs"),
                )
            hw, hs = words_of[(k, c)]
            nc.vector.quantize_mx(
                out=hw[:, lo:hi].bitcast(FP8X4),
                scales=hs[:, lo:hi],
                in_=group_of[(k, c)][:, lo:hi, :].rearrange("p w t -> p (w t)"),
            )

        def layer2(k, r0=0, r1=4):
            if k < 0 or k >= CELLS:
                return
            if r1 - r0 == 4 and k < CELLS - 2:
                acc2 = psum2.tile([P, 4, G1], F32, tag="l2", name="acc2")
            else:
                acc2 = psum1.tile([P, 4, G1], F32, name="acc")
            acc2_of[(k, r0)] = acc2
            for r in range(r0, r1):
                for c in range(2):
                    hw, hs = words_of[(k, c)]
                    nc.tensor.matmul_mx(
                        out=acc2[:, r, :],
                        lhsT=hw[:, r * P : (r + 1) * P].bitcast(FP8X4),
                        lhsT_scale=hs[:, r * P : (r + 1) * P],
                        rhs=w1w[:, c * G1 : (c + 1) * G1].bitcast(FP8X4),
                        rhs_scale=w1s[:, c * G1 : (c + 1) * G1],
                        start=(c == 0),
                        stop=(c == 1),
                    )

        def add_bias(k, r0=0, r1=4):
            if k < 0 or k >= CELLS:
                return
            if r0 == 0:
                ot_of[k] = results.tile([P, 4, G1], F32, name="ot")
            nc.vector.tensor_tensor(
                out=ot_of[k][:, r0:r1, :],
                in0=acc2_of[(k, r0)][:, r0:r1, :],
                in1=b1bc[:].unsqueeze(1).to_broadcast([P, r1 - r0, G1]),
                op=ALU.add,
            )

        outv = out.rearrange("b p q e -> b (p q) e")

        def relu_store(k, lo=0, hi=4):
            if k < 0 or k >= CELLS:
                return
            s = ORDER[k]
            ot = ot_of[k]
            if k >= CELLS - 2:
                nc.scalar.activation(out=ot[:, lo:hi, :], in_=ot[:, lo:hi, :], func=ACT.Relu)
            else:
                nc.vector.tensor_scalar_max(out=ot[:, lo:hi, :], in0=ot[:, lo:hi, :], scalar1=0.0)
            for c in range(4):
                split = min(4, max(0, (CELLS - s - c + 3) // 4))
                for a0, a1, wrap in ((0, split, 0), (split, 4, -256)):
                    r0, r1 = max(a0, lo), min(a1, hi)
                    if r1 <= r0:
                        continue
                    first = 17 * (4 * r0 + c) + 16 * s + wrap
                    nc.sync.dma_start(
                        out=outv[:, first : first + 68 * (r1 - r0 - 1) + 1 : 68, :],
                        in_=ot[B * c : B * (c + 1), r0:r1, :],
                    )

        w0_regroup(nc.vector.tensor_copy, 0, 1)
        nc.vector.tensor_copy(out=bt[:], in_=bt_ps[:, 0:24])
        w0_regroup(nc.vector.tensor_copy, 1, 2)
        bias_rows()
        w0_quantise(0, 2)
        bias_base()
        w0_regroup(nc.vector.tensor_copy, 2, 3)
        xaccs = []
        for i in range(4):
            xacc = psum1.tile([P, COLS], F32, name="acc")
            nc.tensor.matmul(
                out=xacc[:],
                lhsT=spread[i // 2][:],
                rhs=xraw[:, 8 * (i % 2) : 8 * (i % 2) + 8, :].rearrange("p b z -> p (b z)"),
                start=True,
                stop=True,
            )
            xaccs.append(xacc)

        def x_copy(i, h):
            copy = nc.scalar.copy if i % 2 else nc.vector.tensor_copy
            copy(
                out=xg[:, 8 * h : 8 * h + 8, 8 * i : 8 * i + 8, :],
                in_=xaccs[i][:].rearrange("p (b j n) -> p n b j", b=8, j=4)[:, 8 * h : 8 * h + 8],
            )

        def x_quantise(h):
            nc.vector.quantize_mx(
                out=ow2[:, 256 * h : 256 * h + 256].bitcast(FP8X4),
                scales=os2[:, 256 * h : 256 * h + 256],
                in_=xg[:, 8 * h : 8 * h + 8].rearrange("p n b j -> p (n b j)"),
            )

        x_copy(0, 0)
        x_copy(1, 0)
        x_copy(2, 0)
        x_copy(3, 0)
        w0_regroup(nc.vector.tensor_copy, 3, 4)
        x_copy(0, 1)
        x_copy(1, 1)
        x_quantise(0)
        x_copy(2, 1)
        x_copy(3, 1)
        w0_regroup(nc.scalar.copy, 4, 6)
        w0_quantise(2, 4)
        x_quantise(1)
        w0_regroup(nc.vector.tensor_copy, 6, 8)
        bias_table()
        w0_quantise(4, 6)
        w0_quantise(6, 8)
        build_pair(1)
        build_pair(2)

        last = CELLS - 1
        half = COLS // 2
        for k in range(CELLS):
            row_matmul(k, 0)
            layer1(k, 0)
            if k < last:
                regroup(k, 0)
            if k == 0:
                nc.vector.tensor_copy(out=w1g[:], in_=w1raw[:].rearrange("p (c t) n -> p c n t", t=4))
            row_add(k, 0)
            quantise(k - 1, 1)
            row_relu(k, 0)
            layer2(k - 2)
            add_bias(k - 2)
            build_pair(k + 3)
            if k < last:
                layer1(k, 1)
                regroup(k, 1)
                if k == 0:
                    nc.vector.quantize_mx(
                        out=w1w[:].bitcast(FP8X4), scales=w1s[:], in_=w1g[:].rearrange("p c n t -> p (c n t)")
                    )
                row_matmul(k, 1)
                row_add(k, 1)
                quantise(k, 0)
                row_relu(k, 1)
                relu_store(k - 2)

        layer1(last, 1, 2)
        layer2(last - 1)
        regroup(last, 0)
        relu_store(last - 2)
        regroup(last, 1, 0, half)
        regroup(last, 1, half, COLS, nc.scalar.copy)
        add_bias(last - 1)
        relu_store(last - 1)
        quantise(last, 0)
        quantise(last, 1, 0, half)
        layer2(last, 0, 2)
        quantise(last, 1, half, COLS)
        layer2(last, 2, 4)
        add_bias(last, 0, 2)
        relu_store(last, 0, 2)
        add_bias(last, 2, 4)
        relu_store(last, 2, 4)
